import numpy as np
import ml_dtypes


def mxq(x, axis, fmt="e4m3"):
    dtype, down = {"e4m3": (ml_dtypes.float8_e4m3fn, 7), "e5m2": (ml_dtypes.float8_e5m2, 14)}[fmt]
    v = np.moveaxis(np.asarray(x, np.float32).astype(ml_dtypes.bfloat16).astype(np.float64), axis, -1)
    blocks = v.reshape(v.shape[:-1] + (-1, 32))
    amax = np.abs(blocks).max(-1, keepdims=True)
    byte = np.maximum(np.where(amax > 0, np.frexp(amax)[1] - 1 + 127, 0) - down, 1)
    scale = np.exp2(byte - 127.0)
    codes = (blocks / scale).astype(np.float32).astype(dtype).astype(np.float64)
    return np.moveaxis((codes * scale).reshape(v.shape), -1, axis)


WIDE = False


def mx_kscale(k):
    if not WIDE:
        return np.ones(k)
    levels = np.array([10, -10, 5, -5, 0])
    a = np.random.permutation(np.resize(levels, k // 512 * 4)).reshape(k // 512, 4)
    idx = np.arange(k)
    return np.exp2(a[idx // 512, idx % 128 // 32])


BF16 = ml_dtypes.bfloat16


def bf(x):
    return np.asarray(x, np.float32).astype(BF16)


def f64(x):
    return np.asarray(x).astype(np.float64)


E2M1 = np.array([0.0, 0.5, 1.0, 1.5, 2.0, 3.0, 4.0, 6.0, -0.0, -0.5, -1.0, -1.5, -2.0, -3.0, -4.0, -6.0])


def pack_weight(w, fmt):
    k, n = w.shape
    w = f64(bf(w)).reshape(k // 32, 32, n)
    amax = np.abs(w).max(1)
    if fmt == "e4m3":
        byte = np.frexp(amax)[1] - 1 + 127 - 7
    else:
        mant, ex = np.frexp(amax / 6.0)
        byte = np.where(mant > 0.5, ex, ex - 1) + 127
    byte = np.clip(np.where(amax > 0, byte, 1), 1, 254)
    scaled = (w * np.exp2(127.0 - byte)[:, None, :]).reshape(k, n).astype(np.float32)
    by_word = np.ascontiguousarray(scaled.reshape(k // 512, 128, 4, n).transpose(0, 1, 3, 2))
    if fmt == "e4m3":
        words = by_word.astype(ml_dtypes.float8_e4m3fn).view(np.uint8)
    else:
        c = by_word.astype(ml_dtypes.float4_e2m1fn).view(np.uint8) & 0xF
        words = c[..., 0::2] | (c[..., 1::2] << 4)
    return np.ascontiguousarray(words), np.ascontiguousarray(byte.astype(np.uint8).reshape(k // 512, 16, n))


def unpack_weight(words, scales, fmt):
    g, p, n, _ = words.shape
    if fmt == "e4m3":
        vals = np.ascontiguousarray(words).view(ml_dtypes.float8_e4m3fn).astype(np.float64)
    else:
        nib = np.empty((g, p, n, 4), np.uint8)
        nib[..., 0::2] = words & 0xF
        nib[..., 1::2] = words >> 4
        vals = E2M1[nib]
    vals = vals * np.repeat(np.exp2(scales.astype(np.float64) - 127.0), 8, axis=1)[..., None]
    return vals.transpose(0, 1, 3, 2).reshape(g * 512, n)


N, IN_CH, OUT_CH = 1024, 512, 512
K2 = IN_CH + IN_CH
K3 = K2 + IN_CH


def setup_inputs():
    s = mx_kscale(K3)
    q = bf(np.random.standard_normal((N, OUT_CH)) * 2.0)
    k1 = bf(np.random.standard_normal((N, OUT_CH)) * 2.0)
    k2 = bf(np.random.standard_normal((N, OUT_CH)) * 2.0)
    sp = bf(np.random.standard_normal((N, IN_CH)) * s[:IN_CH])
    om1 = bf(np.random.standard_normal((N, IN_CH)) * s[IN_CH:K2])
    om2 = bf(np.random.standard_normal((N, IN_CH)) * s[K2:])
    v_w = np.random.standard_normal((OUT_CH, K3)) * 2.0 / np.sqrt(K3) / s[None, :]
    v_w_words, v_w_scales = pack_weight(np.ascontiguousarray(v_w.T), 'e4m3')
    v_b = bf(np.random.standard_normal(OUT_CH) * 0.3)
    return {
        'q': q,
        'k1': k1,
        'k2': k2,
        'sp': sp,
        'om1': om1,
        'om2': om2,
        'v_w_words': v_w_words,
        'v_w_scales': v_w_scales,
        'v_b': v_b,
    }


def reference(q, k1, k2, sp, om1, om2, v_w_words, v_w_scales, v_b):
    om_cat = np.concatenate([f64(sp), f64(om1), f64(om2)], axis=-1)
    v = (mxq(om_cat, 1, 'e4m3') @ unpack_weight(v_w_words, v_w_scales, 'e4m3')) + f64(v_b)
    vq = mxq(v, 0, 'e4m3')
    scale = 1.0 / np.sqrt(OUT_CH)
    s1 = f64(q) @ f64(k1).T * scale
    s2 = f64(q) @ f64(k2).T * scale
    e1 = np.exp(s1 - s1.max(-1, keepdims=True))
    e2 = np.exp(s2 - s2.max(-1, keepdims=True))
    attn1 = (mxq(e1, 1, 'e4m3') @ vq) / e1.sum(-1, keepdims=True)
    attn2 = (mxq(e2, 1, 'e4m3') @ vq) / e2.sum(-1, keepdims=True)
    return attn1, attn2

@@ -1,0 +1,343 @@
+from contextlib import ExitStack
+import math
+
+import concourse.mybir as mybir
+from concourse.masks import make_identity
+
+BF16 = mybir.dt.bfloat16
+F32 = mybir.dt.float32
+I32 = mybir.dt.int32
+U32 = mybir.dt.uint32
+U8 = mybir.dt.uint8
+FP8X4 = mybir.dt.float8_e4m3fn_x4
+ALU = mybir.AluOpType
+ACT = mybir.ActivationFunctionType
+
+P = 128
+TOKENS = 1024
+WIDTH = 512
+STREAMS = 3
+TILES = TOKENS // P
+CHUNKS = WIDTH // P
+PASSES = TOKENS // 512
+UNITS = 2 * TILES
+SCALE = 1.0 / math.sqrt(WIDTH)
+
+E_LAG = 2
+V_LAG = TILES
+FEATURE_STEPS = 2 * STREAMS
+Q_AHEAD = 2
+
+FLOPS = 2 * TOKENS * STREAMS * WIDTH * WIDTH + 2 * 2 * (2 * TOKENS * TOKENS * WIDTH)
+
+
+def tile_sc_attn_pa_kernel(
+    tc, q, k1, k2, sp, om1, om2, v_w_words, v_w_scales, v_b, out_0, out_1
+):
+    nc = tc.nc
+    outs = (out_0, out_1)
+    with ExitStack() as ctx:
+        keep = ctx.enter_context(tc.tile_pool(name="keep", bufs=1))
+        rotate = ctx.enter_context(tc.tile_pool(name="rotate", bufs=4))
+        score_psum = ctx.enter_context(tc.psum_pool(name="score_psum", bufs=4))
+        work_psum = ctx.enter_context(tc.psum_pool(name="work_psum", bufs=4))
+        ctx.enter_context(tc.manual_schedule())
+
+        ident_bf = keep.tile([P, P], BF16, name="ident_bf")
+        ident_f32 = keep.tile([P, P], F32, name="ident_f32")
+        q_sb = keep.tile([P, TILES, WIDTH], BF16, name="q_sb")
+        k_sb = [keep.tile([P, TILES, WIDTH], BF16, name="k%d_sb" % j) for j in (1, 2)]
+        om_sb = [keep.tile([P, TILES, WIDTH], BF16, name="om%d_sb" % c) for c in range(STREAMS)]
+        qT = keep.tile([P, TILES, CHUNKS, P], BF16, name="qT")
+        kT = [keep.tile([P, CHUNKS, TOKENS], BF16, name="k%dT" % j) for j in (1, 2)]
+        bias_bf = keep.tile([P, WIDTH], BF16, name="bias_bf")
+        w_words = keep.tile([P, STREAMS, WIDTH], U32, name="w_words", align_bytes=64)
+        w_scales = keep.tile([P, STREAMS, WIDTH], U8, name="w_scales", align_bytes=64)
+        x_words = keep.tile([P, STREAMS, TOKENS], U32, name="x_words", align_bytes=64)
+        x_scales = keep.tile([P, STREAMS, TOKENS], U8, name="x_scales", align_bytes=64)
+        v_grouped = keep.tile([P, PASSES, WIDTH, 4], BF16, name="v_grouped", align_bytes=64)
+        v_words = keep.tile([P, PASSES, WIDTH], U32, name="v_words", align_bytes=64)
+        v_scales = keep.tile([P, PASSES, WIDTH], U8, name="v_scales", align_bytes=64)
+        e_words = keep.tile([P, UNITS, PASSES * P], U32, name="e_words", align_bytes=64)
+        e_scales = keep.tile([P, UNITS, PASSES * P], U8, name="e_scales", align_bytes=64)
+        inv_sum = keep.tile([P, UNITS], F32, name="inv_sum")
+
+        make_identity(nc, ident_bf[:])
+        make_identity(nc, ident_f32[:])
+        nc.vector.memset(w_scales[:].bitcast(I32), 0)
+
+        k_views = [k.rearrange("(a p) d -> p a d", p=P) for k in (k1, k2)]
+        for h in range(PASSES):
+            nc.sync.dma_start(out=k_sb[0][:, 4 * h : 4 * h + 4, :], in_=k_views[0][:, 4 * h : 4 * h + 4, :])
+        nc.sync.dma_start(out=q_sb[:], in_=q.rearrange("(i p) d -> p i d", p=P))
+        for c, stream in enumerate((sp, om1, om2)):
+            nc.sync.dma_start(
+                out=om_sb[c][:].rearrange("p (a e) f -> p a e f", e=2),
+                in_=stream.rearrange("(a p e) f -> p a e f", p=P, e=2),
+            )
+        nc.sync.dma_start(
+            out=w_words[:].bitcast(I32),
+            in_=v_w_words.rearrange("c p n t -> p c (n t)").bitcast(I32),
+        )
+        nc.sync.dma_start(out=k_sb[1][:], in_=k_views[1])
+        for quadrant in range(4):
+            nc.sync.dma_start(
+                out=w_scales[32 * quadrant : 32 * quadrant + 4, :, :].bitcast(I32),
+                in_=v_w_scales[:, 4 * quadrant : 4 * quadrant + 4, :].rearrange("c r n -> r c n").bitcast(I32),
+            )
+        nc.sync.dma_start(out=bias_bf[:], in_=v_b.partition_broadcast(P))
+
+        def weave(matmuls, transposes):
+            share = -(-len(transposes) // max(len(matmuls), 1))
+            for m, (out, lhsT, rhs, start, stop) in enumerate(matmuls):
+                nc.tensor.matmul(out, lhsT=lhsT, rhs=rhs, start=start, stop=stop)
+                for t_out, t_in, ident in transposes[m * share : (m + 1) * share]:
+                    nc.tensor.transpose(t_out, t_in, ident)
+            if not matmuls:
+                for t_out, t_in, ident in transposes:
+                    nc.tensor.transpose(t_out, t_in, ident)
+
+        def work_bank(shape, dtype):
+            return work_psum.tile(shape, dtype, name="work_bank", tag="work")
+
+        def key_transposes(j, h):
+            banks = [work_bank([P, 4, P], BF16) for chunk in range(CHUNKS)]
+            calls = [
+                (banks[chunk][:, a, :], k_sb[j][:, 4 * h + a, chunk * P : (chunk + 1) * P], ident_bf[:])
+                for chunk in range(CHUNKS)
+                for a in range(4)
+            ]
+            return banks, calls
+
+        def keep_key_transposes(j, h, banks, copiers):
+            for chunk, bank in enumerate(banks):
+                copiers[chunk % len(copiers)](
+                    out=kT[j][:, chunk, 512 * h : 512 * h + 512],
+                    in_=bank[:].rearrange("p a k -> p (a k)"),
+                )
+
+        def query_transposes(i):
+            bank = work_bank([P, CHUNKS, P], BF16)
+            calls = [
+                (bank[:, chunk, :], q_sb[:, i, chunk * P : (chunk + 1) * P], ident_bf[:])
+                for chunk in range(CHUNKS)
+            ]
+            return bank, calls
+
+        def feature_transposes(c, half):
+            banks = [work_bank([P, 2, 2, P], F32) for b in range(2)]
+            calls = [
+                (
+                    banks[b][:, a, u, :],
+                    om_sb[c][:, 4 * half + 2 * b + a, :].bitcast(F32)[:, u : WIDTH // 2 : 2],
+                    ident_f32[:],
+                )
+                for b in range(2)
+                for a in range(2)
+                for u in range(2)
+            ]
+            return banks, calls
+
+        def regroup_features(banks):
+            grouped = rotate.tile([P, 4 * P * 4], BF16, name="x_grouped", align_bytes=64)
+            words = grouped[:].bitcast(F32).rearrange("p (a k u) -> p a k u", a=4, u=2)
+            for b, bank in enumerate(banks):
+                nc.scalar.copy(
+                    out=words[:, 2 * b : 2 * b + 2, :, :], in_=bank[:].rearrange("p a u k -> p a k u")
+                )
+            return grouped
+
+        def quantise_features(c, half, grouped):
+            columns = slice(512 * half, 512 * half + 512)
+            nc.vector.quantize_mx(
+                out=x_words[:, c, columns].bitcast(FP8X4), scales=x_scales[:, c, columns], in_=grouped[:]
+            )
+
+        def project_values(g):
+            for n in range(CHUNKS):
+                columns = slice(n * P, (n + 1) * P)
+                bank = work_bank([P, 4, P], F32)
+                for t in range(4):
+                    tokens = slice((4 * g + t) * P, (4 * g + t + 1) * P)
+                    for c in range(STREAMS):
+                        nc.tensor.matmul_mx(
+                            out=bank[:, t, :],
+                            lhsT=x_words[:, c, tokens].bitcast(FP8X4),
+                            lhsT_scale=x_scales[:, c, tokens],
+                            rhs=w_words[:, c, columns].bitcast(FP8X4),
+                            rhs_scale=w_scales[:, c, columns],
+                            start=(c == 0),
+                            stop=(c == STREAMS - 1),
+                        )
+                nc.vector.tensor_tensor(
+                    out=v_grouped[:, g, columns, :],
+                    in0=bank[:].rearrange("p t n -> p n t"),
+                    in1=bias_bf[:, columns].unsqueeze(2).to_broadcast([P, P, 4]),
+                    op=ALU.add,
+                )
+
+        def quantise_values(g):
+            nc.vector.quantize_mx(
+                out=v_words[:, g, :].bitcast(FP8X4),
+                scales=v_scales[:, g, :],
+                in_=v_grouped[:, g, :, :].rearrange("p n t -> p (n t)"),
+            )
+
+        score_banks = {}
+        row_max = {}
+        e_rows = {}
+        e_sums = {}
+        e_banks = {}
+        e_grouped = {}
+        products = {}
+
+        def score_matmuls(unit):
+            j, i = divmod(unit, TILES)
+            score_banks[unit] = [
+                score_psum.tile([P, 512], F32, name="score_bank", tag="scores") for h in range(PASSES)
+            ]
+            row_max[unit] = rotate.tile([P, PASSES], F32, name="row_max")
+            return [
+                (
+                    score_banks[unit][h][:],
+                    qT[:, i, chunk, :],
+                    kT[j][:, chunk, 512 * h : 512 * h + 512],
+                    chunk == 0,
+                    chunk == CHUNKS - 1,
+                )
+                for h in range(PASSES)
+                for chunk in range(CHUNKS)
+            ]
+
+        def half_maximum(unit, h):
+            nc.vector.tensor_reduce(
+                out=row_max[unit][:, h : h + 1], in_=score_banks[unit][h][:], axis=mybir.AxisListType.X, op=ALU.max
+            )
+
+        def exponentials(unit):
+            shift = rotate.tile([P, 1], F32, name="shift")
+            nc.vector.tensor_scalar(
+                out=shift[:],
+                in0=row_max[unit][:, 0:1],
+                scalar1=row_max[unit][:, 1:2],
+                scalar2=-SCALE,
+                op0=ALU.max,
+                op1=ALU.mult,
+            )
+            e_rows[unit] = rotate.tile([P, TOKENS], BF16, name="e_rows")
+            e_sums[unit] = rotate.tile([P, PASSES], F32, name="e_sums")
+            for h in range(PASSES):
+                nc.scalar.activation(
+                    out=e_rows[unit][:, 512 * h : 512 * h + 512],
+                    in_=score_banks[unit][h][:],
+                    func=ACT.Exp,
+                    bias=shift[:, 0:1],
+                    scale=SCALE,
+                    accum_out=e_sums[unit][:, h : h + 1],
+                )
+
+        def e_transposes(unit):
+            e_banks[unit] = work_bank([P, 2 * PASSES, P], F32)
+            pairs = e_rows[unit][:].bitcast(F32)
+            return [
+                (e_banks[unit][:, x, :], pairs[:, x * P : (x + 1) * P], ident_f32[:])
+                for x in range(2 * PASSES)
+            ]
+
+        def regroup_e(unit):
+            e_grouped[unit] = rotate.tile([P, PASSES * P * 4], BF16, name="e_grouped", align_bytes=64)
+            nc.vector.tensor_copy(
+                out=e_grouped[unit][:].bitcast(F32).rearrange("p (g m u) -> p g m u", g=PASSES, u=2),
+                in_=e_banks[unit][:].rearrange("p (g u) m -> p g m u", u=2),
+            )
+
+        def quantise_e(unit):
+            nc.vector.quantize_mx(
+                out=e_words[:, unit, :].bitcast(FP8X4), scales=e_scales[:, unit, :], in_=e_grouped[unit][:]
+            )
+            total = rotate.tile([P, 1], F32, name="total")
+            nc.vector.tensor_tensor(
+                out=total[:], in0=e_sums[unit][:, 0:1], in1=e_sums[unit][:, 1:2], op=ALU.add
+            )
+            nc.vector.reciprocal(out=inv_sum[:, unit : unit + 1], in_=total[:])
+
+        def multiply_by_values(unit):
+            products[unit] = work_bank([P, WIDTH], F32)
+            for g in range(PASSES):
+                queries = slice(g * P, (g + 1) * P)
+                nc.tensor.matmul_mx(
+                    out=products[unit][:],
+                    lhsT=e_words[:, unit, queries].bitcast(FP8X4),
+                    lhsT_scale=e_scales[:, unit, queries],
+                    rhs=v_words[:, g, :].bitcast(FP8X4),
+                    rhs_scale=v_scales[:, g, :],
+                    start=(g == 0),
+                    stop=(g == PASSES - 1),
+                )
+
+        def divide_and_store(unit):
+            j, i = divmod(unit, TILES)
+            attn = rotate.tile([P, WIDTH], F32, name="attn")
+            nc.scalar.activation(
+                out=attn[:], in_=products[unit][:], func=ACT.Copy, scale=inv_sum[:, unit : unit + 1]
+            )
+            nc.sync.dma_start(out=outs[j][i * P : (i + 1) * P, :], in_=attn[:])
+
+        both = (nc.vector.tensor_copy, nc.scalar.copy)
+        for h in range(PASSES):
+            banks, calls = key_transposes(0, h)
+            weave([], calls)
+            keep_key_transposes(0, h, banks, both)
+        for i in range(Q_AHEAD):
+            bank, calls = query_transposes(i)
+            weave([], calls)
+            both[i % 2](out=qT[:, i, :, :], in_=bank[:])
+
+        x_grouped = {}
+        for step in range(UNITS + V_LAG):
+            scored = step if step < UNITS else None
+            turned = step - E_LAG if 0 <= step - E_LAG < UNITS else None
+            multiplied = step - V_LAG if step >= V_LAG else None
+            next_query_tile = step + Q_AHEAD if step + Q_AHEAD < TILES else None
+            features = divmod(step, 2) if step < FEATURE_STEPS else None
+            values = step - FEATURE_STEPS if FEATURE_STEPS <= step < FEATURE_STEPS + PASSES else None
+
+            if values is not None:
+                project_values(values)
+            if multiplied is not None:
+                multiply_by_values(multiplied)
+            transposes = []
+            if turned is not None:
+                transposes.extend(e_transposes(turned))
+            if next_query_tile is not None:
+                query_bank, calls = query_transposes(next_query_tile)
+                transposes.extend(calls)
+            if features is not None:
+                feature_banks, calls = feature_transposes(features[0], features[1])
+                transposes.extend(calls)
+            if values is not None:
+                key_banks, calls = key_transposes(1, values)
+                transposes.extend(calls)
+            weave(score_matmuls(scored) if scored is not None else [], transposes)
+
+            if turned is not None:
+                regroup_e(turned)
+            if next_query_tile is not None:
+                nc.scalar.copy(out=qT[:, next_query_tile, :, :], in_=query_bank[:])
+            if scored is not None:
+                half_maximum(scored, 0)
+            if turned is not None:
+                quantise_e(turned)
+            if 1 <= step <= FEATURE_STEPS:
+                c, half = divmod(step - 1, 2)
+                quantise_features(c, half, x_grouped[step - 1])
+            if features is not None:
+                x_grouped[step] = regroup_features(feature_banks)
+            if values is not None:
+                keep_key_transposes(1, values, key_banks, (nc.scalar.copy,))
+                quantise_values(values)
+            if multiplied is not None:
+                divide_and_store(multiplied)
+            if scored is not None:
+                half_maximum(scored, 1)
+                exponentials(scored)

@@ -19,14 +19,17 @@ WIDTH = 512
 STREAMS = 3
 TILES = TOKENS // P
 CHUNKS = WIDTH // P
+WORD_CHUNKS = WIDTH // 2 // P
 PASSES = TOKENS // 512
 UNITS = 2 * TILES
 SCALE = 1.0 / math.sqrt(WIDTH)
 
 E_LAG = 2
-V_LAG = TILES
+FEATURE_START = 2
 FEATURE_STEPS = 2 * STREAMS
-Q_AHEAD = 2
+VALUE_START = FEATURE_START + FEATURE_STEPS
+V_LAG = VALUE_START + PASSES
+LATE_E_LAG = 6
 
 FLOPS = 2 * TOKENS * STREAMS * WIDTH * WIDTH + 2 * 2 * (2 * TOKENS * TOKENS * WIDTH)
 
@@ -39,17 +42,17 @@ def tile_sc_attn_pa_kernel(
     with ExitStack() as ctx:
         keep = ctx.enter_context(tc.tile_pool(name="keep", bufs=1))
         rotate = ctx.enter_context(tc.tile_pool(name="rotate", bufs=4))
+        results = ctx.enter_context(tc.tile_pool(name="results", bufs=V_LAG))
         score_psum = ctx.enter_context(tc.psum_pool(name="score_psum", bufs=4))
         work_psum = ctx.enter_context(tc.psum_pool(name="work_psum", bufs=4))
         ctx.enter_context(tc.manual_schedule())
 
-        ident_bf = keep.tile([P, P], BF16, name="ident_bf")
         ident_f32 = keep.tile([P, P], F32, name="ident_f32")
         q_sb = keep.tile([P, TILES, WIDTH], BF16, name="q_sb")
         k_sb = [keep.tile([P, TILES, WIDTH], BF16, name="k%d_sb" % j) for j in (1, 2)]
         om_sb = [keep.tile([P, TILES, WIDTH], BF16, name="om%d_sb" % c) for c in range(STREAMS)]
-        qT = keep.tile([P, TILES, CHUNKS, P], BF16, name="qT")
-        kT = [keep.tile([P, CHUNKS, TOKENS], BF16, name="k%dT" % j) for j in (1, 2)]
+        qT = keep.tile([P, TILES, WORD_CHUNKS, P, 2], BF16, name="qT")
+        kT = [keep.tile([P, WORD_CHUNKS, TOKENS, 2], BF16, name="k%dT" % j) for j in (1, 2)]
         bias_bf = keep.tile([P, WIDTH], BF16, name="bias_bf")
         w_words = keep.tile([P, STREAMS, WIDTH], U32, name="w_words", align_bytes=64)
         w_scales = keep.tile([P, STREAMS, WIDTH], U8, name="w_scales", align_bytes=64)
@@ -62,14 +65,15 @@ def tile_sc_attn_pa_kernel(
         e_scales = keep.tile([P, UNITS, PASSES * P], U8, name="e_scales", align_bytes=64)
         inv_sum = keep.tile([P, UNITS], F32, name="inv_sum")
 
-        make_identity(nc, ident_bf[:])
         make_identity(nc, ident_f32[:])
         nc.vector.memset(w_scales[:].bitcast(I32), 0)
 
         k_views = [k.rearrange("(a p) d -> p a d", p=P) for k in (k1, k2)]
-        for h in range(PASSES):
-            nc.sync.dma_start(out=k_sb[0][:, 4 * h : 4 * h + 4, :], in_=k_views[0][:, 4 * h : 4 * h + 4, :])
-        nc.sync.dma_start(out=q_sb[:], in_=q.rearrange("(i p) d -> p i d", p=P))
+        q_view = q.rearrange("(i p) d -> p i d", p=P)
+        nc.sync.dma_start(out=q_sb[:, 0:2, :], in_=q_view[:, 0:2, :])
+        nc.sync.dma_start(out=k_sb[0][:, 0:4, :], in_=k_views[0][:, 0:4, :])
+        nc.sync.dma_start(out=k_sb[0][:, 4:TILES, :], in_=k_views[0][:, 4:TILES, :])
+        nc.sync.dma_start(out=q_sb[:, 2:TILES, :], in_=q_view[:, 2:TILES, :])
         for c, stream in enumerate((sp, om1, om2)):
             nc.sync.dma_start(
                 out=om_sb[c][:].rearrange("p (a e) f -> p a e f", e=2),
@@ -101,28 +105,35 @@ def tile_sc_attn_pa_kernel(
             return work_psum.tile(shape, dtype, name="work_bank", tag="work")
 
         def key_transposes(j, h):
-            banks = [work_bank([P, 4, P], BF16) for chunk in range(CHUNKS)]
+            banks = [work_bank([P, 4, P], F32) for x in range(WORD_CHUNKS)]
             calls = [
-                (banks[chunk][:, a, :], k_sb[j][:, 4 * h + a, chunk * P : (chunk + 1) * P], ident_bf[:])
-                for chunk in range(CHUNKS)
+                (banks[x][:, a, :], k_sb[j][:, 4 * h + a, :].bitcast(F32)[:, x * P : (x + 1) * P], ident_f32[:])
+                for x in range(WORD_CHUNKS)
                 for a in range(4)
             ]
             return banks, calls
 
         def keep_key_transposes(j, h, banks, copiers):
-            for chunk, bank in enumerate(banks):
-                copiers[chunk % len(copiers)](
-                    out=kT[j][:, chunk, 512 * h : 512 * h + 512],
-                    in_=bank[:].rearrange("p a k -> p (a k)"),
+            for x, bank in enumerate(banks):
+                copiers[x % len(copiers)](
+                    out=kT[j][:, x, 512 * h : 512 * h + 512, :].rearrange("p k e -> p (k e)"),
+                    in_=bank[:].rearrange("p a k -> p (a k)").bitcast(BF16),
                 )
 
-        def query_transposes(i):
-            bank = work_bank([P, CHUNKS, P], BF16)
+        def query_transposes(pair):
+            bank = work_bank([P, 2, WORD_CHUNKS, P], F32)
             calls = [
-                (bank[:, chunk, :], q_sb[:, i, chunk * P : (chunk + 1) * P], ident_bf[:])
-                for chunk in range(CHUNKS)
+                (bank[:, i, x, :], q_sb[:, 2 * pair + i, :].bitcast(F32)[:, x * P : (x + 1) * P], ident_f32[:])
+                for i in range(2)
+                for x in range(WORD_CHUNKS)
             ]
             return bank, calls
+
+        def keep_query_transposes(pair, bank, copier):
+            copier(
+                out=qT[:, 2 * pair : 2 * pair + 2, :, :, :].rearrange("p i x m e -> p (i x m e)"),
+                in_=bank[:].rearrange("p i x m -> p (i x m)").bitcast(BF16),
+            )
 
         def feature_transposes(c, half):
             banks = [work_bank([P, 2, 2, P], F32) for b in range(2)]
@@ -198,15 +209,18 @@ def tile_sc_attn_pa_kernel(
             ]
             row_max[unit] = rotate.tile([P, PASSES], F32, name="row_max")
             return [
-                (
-                    score_banks[unit][h][:],
-                    qT[:, i, chunk, :],
-                    kT[j][:, chunk, 512 * h : 512 * h + 512],
-                    chunk == 0,
-                    chunk == CHUNKS - 1,
-                )
+                [
+                    (
+                        score_banks[unit][h][:],
+                        qT[:, i, x, :, e],
+                        kT[j][:, x, 512 * h : 512 * h + 512, e],
+                        (x, e) == (0, 0),
+                        (x, e) == (WORD_CHUNKS - 1, 1),
+                    )
+                    for x in range(WORD_CHUNKS)
+                    for e in range(2)
+                ]
                 for h in range(PASSES)
-                for chunk in range(CHUNKS)
             ]
 
         def half_maximum(unit, h):
@@ -275,69 +289,84 @@ def tile_sc_attn_pa_kernel(
                     stop=(g == PASSES - 1),
                 )
 
-        def divide_and_store(unit):
+        def divide_and_store(unit, on_vector):
             j, i = divmod(unit, TILES)
-            attn = rotate.tile([P, WIDTH], F32, name="attn")
-            nc.scalar.activation(
-                out=attn[:], in_=products[unit][:], func=ACT.Copy, scale=inv_sum[:, unit : unit + 1]
-            )
+            attn = results.tile([P, WIDTH], F32, name="attn")
+            if on_vector:
+                nc.vector.tensor_scalar(
+                    out=attn[:], in0=products[unit][:], scalar1=inv_sum[:, unit : unit + 1], scalar2=None, op0=ALU.mult
+                )
+            else:
+                nc.scalar.activation(
+                    out=attn[:], in_=products[unit][:], func=ACT.Copy, scale=inv_sum[:, unit : unit + 1]
+                )
             nc.sync.dma_start(out=outs[j][i * P : (i + 1) * P, :], in_=attn[:])
 
         both = (nc.vector.tensor_copy, nc.scalar.copy)
-        for h in range(PASSES):
-            banks, calls = key_transposes(0, h)
-            weave([], calls)
-            keep_key_transposes(0, h, banks, both)
-        for i in range(Q_AHEAD):
-            bank, calls = query_transposes(i)
-            weave([], calls)
-            both[i % 2](out=qT[:, i, :, :], in_=bank[:])
+        bank, calls = query_transposes(0)
+        weave([], calls)
+        keep_query_transposes(0, bank, nc.vector.tensor_copy)
+        banks, calls = key_transposes(0, 0)
+        weave([], calls)
+        keep_key_transposes(0, 0, banks, both)
 
         x_grouped = {}
         for step in range(UNITS + V_LAG):
             scored = step if step < UNITS else None
-            turned = step - E_LAG if 0 <= step - E_LAG < UNITS else None
             multiplied = step - V_LAG if step >= V_LAG else None
-            next_query_tile = step + Q_AHEAD if step + Q_AHEAD < TILES else None
-            features = divmod(step, 2) if step < FEATURE_STEPS else None
-            values = step - FEATURE_STEPS if FEATURE_STEPS <= step < FEATURE_STEPS + PASSES else None
+            turned = step - E_LAG if E_LAG <= step < UNITS else None
+            if UNITS - E_LAG <= step - LATE_E_LAG < UNITS:
+                turned = step - LATE_E_LAG
+            query_pair = step // 2 + 1 if step % 2 == 0 and step + 2 < TILES else None
+            features = divmod(step - FEATURE_START, 2) if 0 <= step - FEATURE_START < FEATURE_STEPS else None
+            quantised = divmod(step - FEATURE_START - 1, 2) if 0 <= step - FEATURE_START - 1 < FEATURE_STEPS else None
+            values = step - VALUE_START if 0 <= step - VALUE_START < PASSES else None
+            keys = (0, 1) if step == 0 else (1, step - (TILES - PASSES)) if TILES - PASSES <= step < TILES else None
 
+            if quantised is not None:
+                quantise_features(quantised[0], quantised[1], x_grouped[step - 1])
             if values is not None:
                 project_values(values)
             if multiplied is not None:
                 multiply_by_values(multiplied)
-            transposes = []
+            urgent = []
+            patient = []
+            if step == 0:
+                key_banks, calls = key_transposes(keys[0], keys[1])
+                urgent.extend(calls)
             if turned is not None:
-                transposes.extend(e_transposes(turned))
-            if next_query_tile is not None:
-                query_bank, calls = query_transposes(next_query_tile)
-                transposes.extend(calls)
+                urgent.extend(e_transposes(turned))
+            if query_pair is not None:
+                query_bank, calls = query_transposes(query_pair)
+                patient.extend(calls)
             if features is not None:
                 feature_banks, calls = feature_transposes(features[0], features[1])
-                transposes.extend(calls)
-            if values is not None:
-                key_banks, calls = key_transposes(1, values)
-                transposes.extend(calls)
-            weave(score_matmuls(scored) if scored is not None else [], transposes)
+                patient.extend(calls)
+            if keys is not None and step > 0:
+                key_banks, calls = key_transposes(keys[0], keys[1])
+                patient.extend(calls)
+            first_bank, second_bank = score_matmuls(scored) if scored is not None else ([], [])
+            weave(first_bank, urgent)
+            if step == 0:
+                keep_key_transposes(keys[0], keys[1], key_banks, both)
+            weave(second_bank, patient)
 
             if turned is not None:
                 regroup_e(turned)
-            if next_query_tile is not None:
-                nc.scalar.copy(out=qT[:, next_query_tile, :, :], in_=query_bank[:])
+            if values is not None:
+                quantise_values(values)
             if scored is not None:
                 half_maximum(scored, 0)
             if turned is not None:
                 quantise_e(turned)
-            if 1 <= step <= FEATURE_STEPS:
-                c, half = divmod(step - 1, 2)
-                quantise_features(c, half, x_grouped[step - 1])
+            if query_pair is not None:
+                keep_query_transposes(query_pair, query_bank, nc.scalar.copy)
             if features is not None:
                 x_grouped[step] = regroup_features(feature_banks)
-            if values is not None:
-                keep_key_transposes(1, values, key_banks, (nc.scalar.copy,))
-                quantise_values(values)
+            if keys is not None and step > 0:
+                keep_key_transposes(keys[0], keys[1], key_banks, (nc.scalar.copy,))
             if multiplied is not None:
-                divide_and_store(multiplied)
+                divide_and_store(multiplied, on_vector=(UNITS <= step < UNITS + LATE_E_LAG - E_LAG))
             if scored is not None:
                 half_maximum(scored, 1)
                 exponentials(scored)

@@ -24,12 +24,17 @@ PASSES = TOKENS // 512
 UNITS = 2 * TILES
 SCALE = 1.0 / math.sqrt(WIDTH)
 
-E_LAG = 2
-FEATURE_START = 2
+KEY2_START = 1
+FEATURE_START = KEY2_START + PASSES
 FEATURE_STEPS = 2 * STREAMS
 VALUE_START = FEATURE_START + FEATURE_STEPS
 V_LAG = VALUE_START + PASSES
+E_LAG = 2
 LATE_E_LAG = 6
+CATCH_UP = (FEATURE_STEPS + PASSES) // PASSES
+QUANTISES = 2
+SUM_GROUP = 4
+WAITING = FEATURE_STEPS + E_LAG + 2
 
 FLOPS = 2 * TOKENS * STREAMS * WIDTH * WIDTH + 2 * 2 * (2 * TOKENS * TOKENS * WIDTH)
 
@@ -43,6 +48,7 @@ def tile_sc_attn_pa_kernel(
         keep = ctx.enter_context(tc.tile_pool(name="keep", bufs=1))
         rotate = ctx.enter_context(tc.tile_pool(name="rotate", bufs=4))
         results = ctx.enter_context(tc.tile_pool(name="results", bufs=V_LAG))
+        waiting = ctx.enter_context(tc.tile_pool(name="waiting", bufs=WAITING))
         score_psum = ctx.enter_context(tc.psum_pool(name="score_psum", bufs=4))
         work_psum = ctx.enter_context(tc.psum_pool(name="work_psum", bufs=4))
         ctx.enter_context(tc.manual_schedule())
@@ -63,6 +69,7 @@ def tile_sc_attn_pa_kernel(
         v_scales = keep.tile([P, PASSES, WIDTH], U8, name="v_scales", align_bytes=64)
         e_words = keep.tile([P, UNITS, PASSES * P], U32, name="e_words", align_bytes=64)
         e_scales = keep.tile([P, UNITS, PASSES * P], U8, name="e_scales", align_bytes=64)
+        e_sums = keep.tile([P, UNITS, PASSES], F32, name="e_sums")
         inv_sum = keep.tile([P, UNITS], F32, name="inv_sum")
 
         make_identity(nc, ident_f32[:])
@@ -74,6 +81,8 @@ def tile_sc_attn_pa_kernel(
         nc.sync.dma_start(out=k_sb[0][:, 0:4, :], in_=k_views[0][:, 0:4, :])
         nc.sync.dma_start(out=k_sb[0][:, 4:TILES, :], in_=k_views[0][:, 4:TILES, :])
         nc.sync.dma_start(out=q_sb[:, 2:TILES, :], in_=q_view[:, 2:TILES, :])
+        nc.sync.dma_start(out=k_sb[1][:, 0:4, :], in_=k_views[1][:, 0:4, :])
+        nc.sync.dma_start(out=k_sb[1][:, 4:TILES, :], in_=k_views[1][:, 4:TILES, :])
         for c, stream in enumerate((sp, om1, om2)):
             nc.sync.dma_start(
                 out=om_sb[c][:].rearrange("p (a e) f -> p a e f", e=2),
@@ -83,7 +92,6 @@ def tile_sc_attn_pa_kernel(
             out=w_words[:].bitcast(I32),
             in_=v_w_words.rearrange("c p n t -> p c (n t)").bitcast(I32),
         )
-        nc.sync.dma_start(out=k_sb[1][:], in_=k_views[1])
         for quadrant in range(4):
             nc.sync.dma_start(
                 out=w_scales[32 * quadrant : 32 * quadrant + 4, :, :].bitcast(I32),
@@ -92,11 +100,12 @@ def tile_sc_attn_pa_kernel(
         nc.sync.dma_start(out=bias_bf[:], in_=v_b.partition_broadcast(P))
 
         def weave(matmuls, transposes):
-            share = -(-len(transposes) // max(len(matmuls), 1))
+            gaps = max(len(matmuls) - 1, 1)
             for m, (out, lhsT, rhs, start, stop) in enumerate(matmuls):
                 nc.tensor.matmul(out, lhsT=lhsT, rhs=rhs, start=start, stop=stop)
-                for t_out, t_in, ident in transposes[m * share : (m + 1) * share]:
-                    nc.tensor.transpose(t_out, t_in, ident)
+                for n, (t_out, t_in, ident) in enumerate(transposes):
+                    if n * gaps // len(transposes) == m:
+                        nc.tensor.transpose(t_out, t_in, ident)
             if not matmuls:
                 for t_out, t_in, ident in transposes:
                     nc.tensor.transpose(t_out, t_in, ident)
@@ -152,11 +161,10 @@ def tile_sc_attn_pa_kernel(
         def regroup_features(banks):
             grouped = rotate.tile([P, 4 * P * 4], BF16, name="x_grouped", align_bytes=64)
             words = grouped[:].bitcast(F32).rearrange("p (a k u) -> p a k u", a=4, u=2)
-            for b, bank in enumerate(banks):
-                nc.scalar.copy(
-                    out=words[:, 2 * b : 2 * b + 2, :, :], in_=bank[:].rearrange("p a u k -> p a k u")
-                )
-            return grouped
+            return grouped, [
+                (words[:, 2 * b : 2 * b + 2, :, :], bank[:].rearrange("p a u k -> p a k u"))
+                for b, bank in enumerate(banks)
+            ]
 
         def quantise_features(c, half, grouped):
             columns = slice(512 * half, 512 * half + 512)
@@ -197,7 +205,6 @@ def tile_sc_attn_pa_kernel(
         score_banks = {}
         row_max = {}
         e_rows = {}
-        e_sums = {}
         e_banks = {}
         e_grouped = {}
         products = {}
@@ -238,8 +245,7 @@ def tile_sc_attn_pa_kernel(
                 op0=ALU.max,
                 op1=ALU.mult,
             )
-            e_rows[unit] = rotate.tile([P, TOKENS], BF16, name="e_rows")
-            e_sums[unit] = rotate.tile([P, PASSES], F32, name="e_sums")
+            e_rows[unit] = waiting.tile([P, TOKENS], BF16, name="e_rows")
             for h in range(PASSES):
                 nc.scalar.activation(
                     out=e_rows[unit][:, 512 * h : 512 * h + 512],
@@ -247,7 +253,7 @@ def tile_sc_attn_pa_kernel(
                     func=ACT.Exp,
                     bias=shift[:, 0:1],
                     scale=SCALE,
-                    accum_out=e_sums[unit][:, h : h + 1],
+                    accum_out=e_sums[:, unit, h : h + 1],
                 )
 
         def e_transposes(unit):
@@ -258,9 +264,9 @@ def tile_sc_attn_pa_kernel(
                 for x in range(2 * PASSES)
             ]
 
-        def regroup_e(unit):
-            e_grouped[unit] = rotate.tile([P, PASSES * P * 4], BF16, name="e_grouped", align_bytes=64)
-            nc.vector.tensor_copy(
+        def regroup_e(unit, copier):
+            e_grouped[unit] = waiting.tile([P, PASSES * P * 4], BF16, name="e_grouped", align_bytes=64)
+            copier(
                 out=e_grouped[unit][:].bitcast(F32).rearrange("p (g m u) -> p g m u", g=PASSES, u=2),
                 in_=e_banks[unit][:].rearrange("p (g u) m -> p g m u", u=2),
             )
@@ -269,11 +275,11 @@ def tile_sc_attn_pa_kernel(
             nc.vector.quantize_mx(
                 out=e_words[:, unit, :].bitcast(FP8X4), scales=e_scales[:, unit, :], in_=e_grouped[unit][:]
             )
-            total = rotate.tile([P, 1], F32, name="total")
-            nc.vector.tensor_tensor(
-                out=total[:], in0=e_sums[unit][:, 0:1], in1=e_sums[unit][:, 1:2], op=ALU.add
-            )
-            nc.vector.reciprocal(out=inv_sum[:, unit : unit + 1], in_=total[:])
+
+        def invert_sums(units):
+            total = rotate.tile([P, SUM_GROUP], F32, name="total")
+            nc.vector.tensor_reduce(out=total[:], in_=e_sums[:, units, :], axis=mybir.AxisListType.X, op=ALU.add)
+            nc.vector.reciprocal(out=inv_sum[:, units], in_=total[:])
 
         def multiply_by_values(unit):
             products[unit] = work_bank([P, WIDTH], F32)
@@ -311,17 +317,21 @@ def tile_sc_attn_pa_kernel(
         keep_key_transposes(0, 0, banks, both)
 
         x_grouped = {}
+        turned_so_far = 0
+        regrouped = []
+        inverted_so_far = 0
         for step in range(UNITS + V_LAG):
             scored = step if step < UNITS else None
             multiplied = step - V_LAG if step >= V_LAG else None
-            turned = step - E_LAG if E_LAG <= step < UNITS else None
-            if UNITS - E_LAG <= step - LATE_E_LAG < UNITS:
-                turned = step - LATE_E_LAG
             query_pair = step // 2 + 1 if step % 2 == 0 and step + 2 < TILES else None
+            keys = (0, 1) if step == 0 else (1, step - KEY2_START) if 0 <= step - KEY2_START < PASSES else None
             features = divmod(step - FEATURE_START, 2) if 0 <= step - FEATURE_START < FEATURE_STEPS else None
             quantised = divmod(step - FEATURE_START - 1, 2) if 0 <= step - FEATURE_START - 1 < FEATURE_STEPS else None
             values = step - VALUE_START if 0 <= step - VALUE_START < PASSES else None
-            keys = (0, 1) if step == 0 else (1, step - (TILES - PASSES)) if TILES - PASSES <= step < TILES else None
+            done_e = step - (E_LAG if step < UNITS else LATE_E_LAG)
+            most = 0 if features is not None else CATCH_UP if values is not None else 1
+            turned = list(range(turned_so_far, min(turned_so_far + most, done_e + 1, UNITS)))
+            turned_so_far += len(turned)
 
             if quantised is not None:
                 quantise_features(quantised[0], quantised[1], x_grouped[step - 1])
@@ -329,44 +339,50 @@ def tile_sc_attn_pa_kernel(
                 project_values(values)
             if multiplied is not None:
                 multiply_by_values(multiplied)
-            urgent = []
-            patient = []
-            if step == 0:
-                key_banks, calls = key_transposes(keys[0], keys[1])
-                urgent.extend(calls)
-            if turned is not None:
-                urgent.extend(e_transposes(turned))
-            if query_pair is not None:
-                query_bank, calls = query_transposes(query_pair)
-                patient.extend(calls)
+            transposes = []
+            if keys is not None:
+                key_banks, key_calls = key_transposes(keys[0], keys[1])
+            if keys is not None and step > 0:
+                transposes.extend(key_calls)
+            for unit in turned:
+                transposes.extend(e_transposes(unit))
             if features is not None:
                 feature_banks, calls = feature_transposes(features[0], features[1])
-                patient.extend(calls)
-            if keys is not None and step > 0:
-                key_banks, calls = key_transposes(keys[0], keys[1])
-                patient.extend(calls)
+                transposes.extend(calls)
+            if query_pair is not None:
+                query_bank, calls = query_transposes(query_pair)
+                transposes.extend(calls)
             first_bank, second_bank = score_matmuls(scored) if scored is not None else ([], [])
-            weave(first_bank, urgent)
             if step == 0:
+                weave(first_bank, key_calls)
                 keep_key_transposes(keys[0], keys[1], key_banks, both)
-            weave(second_bank, patient)
+                weave(second_bank, transposes)
+            else:
+                weave(first_bank + second_bank, transposes)
 
-            if turned is not None:
-                regroup_e(turned)
             if values is not None:
                 quantise_values(values)
-            if scored is not None:
-                half_maximum(scored, 0)
-            if turned is not None:
-                quantise_e(turned)
-            if query_pair is not None:
-                keep_query_transposes(query_pair, query_bank, nc.scalar.copy)
-            if features is not None:
-                x_grouped[step] = regroup_features(feature_banks)
-            if keys is not None and step > 0:
-                keep_key_transposes(keys[0], keys[1], key_banks, (nc.scalar.copy,))
+            for unit in regrouped[:QUANTISES]:
+                quantise_e(unit)
+            regrouped = regrouped[QUANTISES:] + turned
+            if inverted_so_far + SUM_GROUP <= min(done_e + 1, UNITS):
+                invert_sums(slice(inverted_so_far, inverted_so_far + SUM_GROUP))
+                inverted_so_far += SUM_GROUP
             if multiplied is not None:
                 divide_and_store(multiplied, on_vector=(UNITS <= step < UNITS + LATE_E_LAG - E_LAG))
+            if keys is not None and step > 0:
+                keep_key_transposes(keys[0], keys[1], key_banks, both)
+            if scored is not None:
+                half_maximum(scored, 0)
+            for unit in turned:
+                regroup_e(unit, nc.scalar.copy if values is not None else nc.vector.tensor_copy)
+            if features is not None:
+                x_grouped[step], copies = regroup_features(feature_banks)
+                nc.scalar.copy(out=copies[0][0], in_=copies[0][1])
+            if query_pair is not None:
+                keep_query_transposes(query_pair, query_bank, nc.scalar.copy)
             if scored is not None:
                 half_maximum(scored, 1)
                 exponentials(scored)
+            if features is not None:
+                nc.vector.tensor_copy(out=copies[1][0], in_=copies[1][1])

@@ -57,7 +57,7 @@ def tile_sc_attn_pa_kernel(
         q_sb = keep.tile([P, TILES, WIDTH], BF16, name="q_sb")
         k_sb = [keep.tile([P, TILES, WIDTH], BF16, name="k%d_sb" % j) for j in (1, 2)]
         om_sb = [keep.tile([P, TILES, WIDTH], BF16, name="om%d_sb" % c) for c in range(STREAMS)]
-        qT = keep.tile([P, TILES, WORD_CHUNKS, P, 2], BF16, name="qT")
+        qT = keep.tile([P, TILES, WORD_CHUNKS, 2, P], BF16, name="qT")
         kT = [keep.tile([P, WORD_CHUNKS, TOKENS, 2], BF16, name="k%dT" % j) for j in (1, 2)]
         bias_bf = keep.tile([P, WIDTH], BF16, name="bias_bf")
         w_words = keep.tile([P, STREAMS, WIDTH], U32, name="w_words", align_bytes=64)
@@ -140,8 +140,8 @@ def tile_sc_attn_pa_kernel(
 
         def keep_query_transposes(pair, bank, copier):
             copier(
-                out=qT[:, 2 * pair : 2 * pair + 2, :, :, :].rearrange("p i x m e -> p (i x m e)"),
-                in_=bank[:].rearrange("p i x m -> p (i x m)").bitcast(BF16),
+                out=qT[:, 2 * pair : 2 * pair + 2, :, :, :].rearrange("p i x e m -> p (i x) e m"),
+                in_=bank[:].rearrange("p i x m -> p (i x m)").bitcast(BF16).rearrange("p (c m e) -> p c e m", m=P, e=2),
             )
 
         def feature_transposes(c, half):
@@ -219,7 +219,7 @@ def tile_sc_attn_pa_kernel(
                 [
                     (
                         score_banks[unit][h][:],
-                        qT[:, i, x, :, e],
+                        qT[:, i, x, e, :],
                         kT[j][:, x, 512 * h : 512 * h + 512, e],
                         (x, e) == (0, 0),
                         (x, e) == (WORD_CHUNKS - 1, 1),

@@ -54,6 +54,7 @@ def tile_sc_attn_pa_kernel(
         ctx.enter_context(tc.manual_schedule())
 
         ident_f32 = keep.tile([P, P], F32, name="ident_f32")
+        zeros = keep.tile([P, WIDTH], BF16, name="zeros")
         q_sb = keep.tile([P, TILES, WIDTH], BF16, name="q_sb")
         k_sb = [keep.tile([P, TILES, WIDTH], BF16, name="k%d_sb" % j) for j in (1, 2)]
         om_sb = [keep.tile([P, TILES, WIDTH], BF16, name="om%d_sb" % c) for c in range(STREAMS)]
@@ -72,6 +73,7 @@ def tile_sc_attn_pa_kernel(
         e_sums = keep.tile([P, UNITS, PASSES], F32, name="e_sums")
         inv_sum = keep.tile([P, UNITS], F32, name="inv_sum")
 
+        nc.vector.memset(zeros[:], 0.0)
         make_identity(nc, ident_f32[:])
         nc.vector.memset(w_scales[:].bitcast(I32), 0)
 
@@ -309,12 +311,21 @@ def tile_sc_attn_pa_kernel(
             nc.sync.dma_start(out=outs[j][i * P : (i + 1) * P, :], in_=attn[:])
 
         both = (nc.vector.tensor_copy, nc.scalar.copy)
+        warm_bank = score_psum.tile([P, 512], F32, name="warm_bank", tag="scores")
+
+        def warm_up(count):
+            for repeat in range(count):
+                nc.tensor.matmul(warm_bank[:], lhsT=zeros[:, 0:P], rhs=zeros[:], start=True, stop=True)
+
+        warm_up(4)
         bank, calls = query_transposes(0)
         weave([], calls)
         keep_query_transposes(0, bank, nc.vector.tensor_copy)
+        warm_up(2)
         banks, calls = key_transposes(0, 0)
         weave([], calls)
         keep_key_transposes(0, 0, banks, both)
+        warm_up(3)
 
         x_grouped = {}
         turned_so_far = 0

@@ -34,6 +34,11 @@ LATE_E_LAG = 6
 CATCH_UP = (FEATURE_STEPS + PASSES) // PASSES
 QUANTISES = 2
 SUM_GROUP = 4
+WARM = 6
+LAST_PARTS = 2
+V_LATE = 22
+HEAD_TILES = 3
+QUERIES = {0: [2, 3], 2: [4, 5], 4: [6, 7]}
 WAITING = FEATURE_STEPS + E_LAG + 2
 
 FLOPS = 2 * TOKENS * STREAMS * WIDTH * WIDTH + 2 * 2 * (2 * TOKENS * TOKENS * WIDTH)
@@ -79,10 +84,12 @@ def tile_sc_attn_pa_kernel(
 
         k_views = [k.rearrange("(a p) d -> p a d", p=P) for k in (k1, k2)]
         q_view = q.rearrange("(i p) d -> p i d", p=P)
+        nc.sync.dma_start(out=k_sb[0][:, 0:1, :], in_=k_views[0][:, 0:1, :])
         nc.sync.dma_start(out=q_sb[:, 0:2, :], in_=q_view[:, 0:2, :])
-        nc.sync.dma_start(out=k_sb[0][:, 0:4, :], in_=k_views[0][:, 0:4, :])
-        nc.sync.dma_start(out=k_sb[0][:, 4:TILES, :], in_=k_views[0][:, 4:TILES, :])
-        nc.sync.dma_start(out=q_sb[:, 2:TILES, :], in_=q_view[:, 2:TILES, :])
+        for a in range(1, TILES):
+            nc.sync.dma_start(out=k_sb[0][:, a : a + 1, :], in_=k_views[0][:, a : a + 1, :])
+        nc.sync.dma_start(out=q_sb[:, 2:4, :], in_=q_view[:, 2:4, :])
+        nc.sync.dma_start(out=q_sb[:, 4:TILES, :], in_=q_view[:, 4:TILES, :])
         nc.sync.dma_start(out=k_sb[1][:, 0:4, :], in_=k_views[1][:, 0:4, :])
         nc.sync.dma_start(out=k_sb[1][:, 4:TILES, :], in_=k_views[1][:, 4:TILES, :])
         for c, stream in enumerate((sp, om1, om2)):
@@ -131,18 +138,29 @@ def tile_sc_attn_pa_kernel(
                     in_=bank[:].rearrange("p a k -> p (a k)").bitcast(BF16),
                 )
 
-        def query_transposes(pair):
-            bank = work_bank([P, 2, WORD_CHUNKS, P], F32)
+        def transpose_key_tile(a, copier):
+            bank = work_bank([P, WORD_CHUNKS, P], F32)
+            for x in range(WORD_CHUNKS):
+                nc.tensor.transpose(
+                    bank[:, x, :], k_sb[0][:, a, :].bitcast(F32)[:, x * P : (x + 1) * P], ident_f32[:]
+                )
+            copier(
+                out=kT[0][:, :, a * P : (a + 1) * P, :].rearrange("p x k e -> p x (k e)"),
+                in_=bank[:].rearrange("p x k -> p (x k)").bitcast(BF16).rearrange("p (x k) -> p x k", x=WORD_CHUNKS),
+            )
+
+        def query_transposes(tiles):
+            bank = work_bank([P, len(tiles), WORD_CHUNKS, P], F32)
             calls = [
-                (bank[:, i, x, :], q_sb[:, 2 * pair + i, :].bitcast(F32)[:, x * P : (x + 1) * P], ident_f32[:])
-                for i in range(2)
+                (bank[:, n, x, :], q_sb[:, i, :].bitcast(F32)[:, x * P : (x + 1) * P], ident_f32[:])
+                for n, i in enumerate(tiles)
                 for x in range(WORD_CHUNKS)
             ]
             return bank, calls
 
-        def keep_query_transposes(pair, bank, copier):
+        def keep_query_transposes(tiles, bank, copier):
             copier(
-                out=qT[:, 2 * pair : 2 * pair + 2, :, :, :].rearrange("p i x e m -> p (i x) e m"),
+                out=qT[:, tiles[0] : tiles[-1] + 1, :, :, :].rearrange("p i x e m -> p (i x) e m"),
                 in_=bank[:].rearrange("p i x m -> p (i x m)").bitcast(BF16).rearrange("p (c m e) -> p c e m", m=P, e=2),
             )
 
@@ -211,25 +229,23 @@ def tile_sc_attn_pa_kernel(
         e_grouped = {}
         products = {}
 
-        def score_matmuls(unit):
+        def score_matmuls(unit, width=512):
             j, i = divmod(unit, TILES)
             score_banks[unit] = [
                 score_psum.tile([P, 512], F32, name="score_bank", tag="scores") for h in range(PASSES)
             ]
             row_max[unit] = rotate.tile([P, PASSES], F32, name="row_max")
             return [
-                [
-                    (
-                        score_banks[unit][h][:],
-                        qT[:, i, x, e, :],
-                        kT[j][:, x, 512 * h : 512 * h + 512, e],
-                        (x, e) == (0, 0),
-                        (x, e) == (WORD_CHUNKS - 1, 1),
-                    )
-                    for x in range(WORD_CHUNKS)
-                    for e in range(2)
-                ]
-                for h in range(PASSES)
+                (
+                    score_banks[unit][start // 512][:, start % 512 : start % 512 + width],
+                    qT[:, i, x, e, :],
+                    kT[j][:, x, start : start + width, e],
+                    (x, e) == (0, 0),
+                    (x, e) == (WORD_CHUNKS - 1, 1),
+                )
+                for start in range(0, TOKENS, width)
+                for x in range(WORD_CHUNKS)
+                for e in range(2)
             ]
 
         def half_maximum(unit, h):
@@ -283,49 +299,54 @@ def tile_sc_attn_pa_kernel(
             nc.vector.tensor_reduce(out=total[:], in_=e_sums[:, units, :], axis=mybir.AxisListType.X, op=ALU.add)
             nc.vector.reciprocal(out=inv_sum[:, units], in_=total[:])
 
-        def multiply_by_values(unit):
-            products[unit] = work_bank([P, WIDTH], F32)
-            for g in range(PASSES):
-                queries = slice(g * P, (g + 1) * P)
-                nc.tensor.matmul_mx(
-                    out=products[unit][:],
-                    lhsT=e_words[:, unit, queries].bitcast(FP8X4),
-                    lhsT_scale=e_scales[:, unit, queries],
-                    rhs=v_words[:, g, :].bitcast(FP8X4),
-                    rhs_scale=v_scales[:, g, :],
-                    start=(g == 0),
-                    stop=(g == PASSES - 1),
-                )
+        def multiply_by_values(unit, parts):
+            width = WIDTH // parts
+            products[unit] = []
+            for n in range(parts):
+                columns = slice(n * width, (n + 1) * width)
+                bank = work_bank([P, WIDTH], F32)
+                products[unit].append((columns, bank))
+                for g in range(PASSES):
+                    queries = slice(g * P, (g + 1) * P)
+                    nc.tensor.matmul_mx(
+                        out=bank[:, 0:width],
+                        lhsT=e_words[:, unit, queries].bitcast(FP8X4),
+                        lhsT_scale=e_scales[:, unit, queries],
+                        rhs=v_words[:, g, columns].bitcast(FP8X4),
+                        rhs_scale=v_scales[:, g, columns],
+                        start=(g == 0),
+                        stop=(g == PASSES - 1),
+                    )
 
         def divide_and_store(unit, on_vector):
             j, i = divmod(unit, TILES)
-            attn = results.tile([P, WIDTH], F32, name="attn")
-            if on_vector:
-                nc.vector.tensor_scalar(
-                    out=attn[:], in0=products[unit][:], scalar1=inv_sum[:, unit : unit + 1], scalar2=None, op0=ALU.mult
-                )
-            else:
-                nc.scalar.activation(
-                    out=attn[:], in_=products[unit][:], func=ACT.Copy, scale=inv_sum[:, unit : unit + 1]
-                )
-            nc.sync.dma_start(out=outs[j][i * P : (i + 1) * P, :], in_=attn[:])
+            for n, (columns, bank) in enumerate(products[unit]):
+                width = columns.stop - columns.start
+                attn = results.tile([P, WIDTH], F32, name="attn")
+                if on_vector == (n == 0):
+                    nc.vector.tensor_scalar(
+                        out=attn[:, 0:width],
+                        in0=bank[:, 0:width],
+                        scalar1=inv_sum[:, unit : unit + 1],
+                        scalar2=None,
+                        op0=ALU.mult,
+                    )
+                else:
+                    nc.scalar.activation(
+                        out=attn[:, 0:width], in_=bank[:, 0:width], func=ACT.Copy, scale=inv_sum[:, unit : unit + 1]
+                    )
+                nc.sync.dma_start(out=outs[j][i * P : (i + 1) * P, columns], in_=attn[:, 0:width])
 
         both = (nc.vector.tensor_copy, nc.scalar.copy)
-        warm_bank = score_psum.tile([P, 512], F32, name="warm_bank", tag="scores")
-
-        def warm_up(count):
-            for repeat in range(count):
-                nc.tensor.matmul(warm_bank[:], lhsT=zeros[:, 0:P], rhs=zeros[:], start=True, stop=True)
-
-        warm_up(4)
-        bank, calls = query_transposes(0)
-        weave([], calls)
-        keep_query_transposes(0, bank, nc.vector.tensor_copy)
-        warm_up(2)
-        banks, calls = key_transposes(0, 0)
-        weave([], calls)
-        keep_key_transposes(0, 0, banks, both)
-        warm_up(3)
+        warm_bank = work_bank([P, WIDTH], F32)
+        for repeat in range(WARM):
+            nc.tensor.matmul(warm_bank[:], lhsT=zeros[:, 0:P], rhs=zeros[:], start=True, stop=True)
+        transpose_key_tile(0, nc.vector.tensor_copy)
+        for i in range(2):
+            bank, calls = query_transposes([i])
+            weave([], calls)
+            keep_query_transposes([i], bank, nc.scalar.copy)
+            transpose_key_tile(i + 1, both[i % 2])
 
         x_grouped = {}
         turned_so_far = 0
@@ -334,8 +355,8 @@ def tile_sc_attn_pa_kernel(
         for step in range(UNITS + V_LAG):
             scored = step if step < UNITS else None
             multiplied = step - V_LAG if step >= V_LAG else None
-            query_pair = step // 2 + 1 if step % 2 == 0 and step + 2 < TILES else None
-            keys = (0, 1) if step == 0 else (1, step - KEY2_START) if 0 <= step - KEY2_START < PASSES else None
+            queries = QUERIES.get(step)
+            keys = (1, step - KEY2_START) if 0 <= step - KEY2_START < PASSES else None
             features = divmod(step - FEATURE_START, 2) if 0 <= step - FEATURE_START < FEATURE_STEPS else None
             quantised = divmod(step - FEATURE_START - 1, 2) if 0 <= step - FEATURE_START - 1 < FEATURE_STEPS else None
             values = step - VALUE_START if 0 <= step - VALUE_START < PASSES else None
@@ -349,27 +370,30 @@ def tile_sc_attn_pa_kernel(
             if values is not None:
                 project_values(values)
             if multiplied is not None:
-                multiply_by_values(multiplied)
+                multiply_by_values(multiplied, LAST_PARTS if multiplied == UNITS - 1 else 1)
             transposes = []
             if keys is not None:
                 key_banks, key_calls = key_transposes(keys[0], keys[1])
-            if keys is not None and step > 0:
                 transposes.extend(key_calls)
             for unit in turned:
                 transposes.extend(e_transposes(unit))
             if features is not None:
                 feature_banks, calls = feature_transposes(features[0], features[1])
                 transposes.extend(calls)
-            if query_pair is not None:
-                query_bank, calls = query_transposes(query_pair)
+            if queries is not None:
+                query_bank, calls = query_transposes(queries)
                 transposes.extend(calls)
-            first_bank, second_bank = score_matmuls(scored) if scored is not None else ([], [])
             if step == 0:
-                weave(first_bank, key_calls)
-                keep_key_transposes(keys[0], keys[1], key_banks, both)
-                weave(second_bank, transposes)
+                matmuls = score_matmuls(0, P)
+                for a in range(TILES):
+                    if a + HEAD_TILES < TILES:
+                        weave(matmuls[4 * a : 4 * a + 4], [])
+                        transpose_key_tile(a + HEAD_TILES, both[(a + HEAD_TILES) % 2])
+                    else:
+                        rest = a - (TILES - HEAD_TILES)
+                        weave(matmuls[4 * a : 4 * a + 4], transposes if rest == 0 else [])
             else:
-                weave(first_bank + second_bank, transposes)
+                weave(score_matmuls(scored) if scored is not None else [], transposes)
 
             if values is not None:
                 quantise_values(values)
@@ -380,8 +404,8 @@ def tile_sc_attn_pa_kernel(
                 invert_sums(slice(inverted_so_far, inverted_so_far + SUM_GROUP))
                 inverted_so_far += SUM_GROUP
             if multiplied is not None:
-                divide_and_store(multiplied, on_vector=(UNITS <= step < UNITS + LATE_E_LAG - E_LAG))
-            if keys is not None and step > 0:
+                divide_and_store(multiplied, on_vector=(UNITS <= step < UNITS + LATE_E_LAG - E_LAG or (step > V_LATE and step % 2 == 0)))
+            if keys is not None:
                 keep_key_transposes(keys[0], keys[1], key_banks, both)
             if scored is not None:
                 half_maximum(scored, 0)
@@ -390,8 +414,8 @@ def tile_sc_attn_pa_kernel(
             if features is not None:
                 x_grouped[step], copies = regroup_features(feature_banks)
                 nc.scalar.copy(out=copies[0][0], in_=copies[0][1])
-            if query_pair is not None:
-                keep_query_transposes(query_pair, query_bank, nc.scalar.copy)
+            if queries is not None:
+                keep_query_transposes(queries, query_bank, nc.scalar.copy)
             if scored is not None:
                 half_maximum(scored, 1)
                 exponentials(scored)

@@ -24,21 +24,24 @@ PASSES = TOKENS // 512
 UNITS = 2 * TILES
 SCALE = 1.0 / math.sqrt(WIDTH)
 
-KEY2_START = 1
-FEATURE_START = KEY2_START + PASSES
+FEATURE_START = 3
+KEY2_STEPS = (4, 5, 6, 7)
+X_ON_SCALAR = (3, 4, 5, 6, 7, 8)
+K2_QUEUE = "scalar"
 FEATURE_STEPS = 2 * STREAMS
 VALUE_START = FEATURE_START + FEATURE_STEPS
 V_LAG = VALUE_START + PASSES
 E_LAG = 2
-LATE_E_LAG = 6
+LATE_E_LAG = 5
 CATCH_UP = (FEATURE_STEPS + PASSES) // PASSES
 QUANTISES = 2
 SUM_GROUP = 4
 WARM = 6
 LAST_PARTS = 2
-V_LATE = 22
+V_LATE = 23
+LEAD = True
 HEAD_TILES = 3
-QUERIES = {0: [2, 3], 2: [4, 5], 4: [6, 7]}
+QUERIES = {0: [2, 3], 1: [4, 5], 2: [6, 7]}
 WAITING = FEATURE_STEPS + E_LAG + 2
 
 FLOPS = 2 * TOKENS * STREAMS * WIDTH * WIDTH + 2 * 2 * (2 * TOKENS * TOKENS * WIDTH)
@@ -61,10 +64,12 @@ def tile_sc_attn_pa_kernel(
         ident_f32 = keep.tile([P, P], F32, name="ident_f32")
         zeros = keep.tile([P, WIDTH], BF16, name="zeros")
         q_sb = keep.tile([P, TILES, WIDTH], BF16, name="q_sb")
-        k_sb = [keep.tile([P, TILES, WIDTH], BF16, name="k%d_sb" % j) for j in (1, 2)]
+        k1_sb = keep.tile([P, TILES, WIDTH], BF16, name="k1_sb")
+        k2_blocks = keep.tile([P, WORD_CHUNKS, TOKENS // 32, 64], BF16, name="k2_blocks", align_bytes=64)
         om_sb = [keep.tile([P, TILES, WIDTH], BF16, name="om%d_sb" % c) for c in range(STREAMS)]
         qT = keep.tile([P, TILES, WORD_CHUNKS, 2, P], BF16, name="qT")
-        kT = [keep.tile([P, WORD_CHUNKS, TOKENS, 2], BF16, name="k%dT" % j) for j in (1, 2)]
+        k1T = keep.tile([P, TILES, WORD_CHUNKS, P, 2], BF16, name="k1T")
+        k2T = keep.tile([P, WORD_CHUNKS, TOKENS, 2], BF16, name="k2T", align_bytes=64)
         bias_bf = keep.tile([P, WIDTH], BF16, name="bias_bf")
         w_words = keep.tile([P, STREAMS, WIDTH], U32, name="w_words", align_bytes=64)
         w_scales = keep.tile([P, STREAMS, WIDTH], U8, name="w_scales", align_bytes=64)
@@ -82,16 +87,15 @@ def tile_sc_attn_pa_kernel(
         make_identity(nc, ident_f32[:])
         nc.vector.memset(w_scales[:].bitcast(I32), 0)
 
-        k_views = [k.rearrange("(a p) d -> p a d", p=P) for k in (k1, k2)]
+        k1_view = k1.rearrange("(a p) d -> p a d", p=P)
+        k2_lanes = k2.rearrange("(r j) d -> j r d", j=32)
         q_view = q.rearrange("(i p) d -> p i d", p=P)
-        nc.sync.dma_start(out=k_sb[0][:, 0:1, :], in_=k_views[0][:, 0:1, :])
+        nc.sync.dma_start(out=k1_sb[:, 0:1, :], in_=k1_view[:, 0:1, :])
         nc.sync.dma_start(out=q_sb[:, 0:2, :], in_=q_view[:, 0:2, :])
         for a in range(1, TILES):
-            nc.sync.dma_start(out=k_sb[0][:, a : a + 1, :], in_=k_views[0][:, a : a + 1, :])
+            nc.sync.dma_start(out=k1_sb[:, a : a + 1, :], in_=k1_view[:, a : a + 1, :])
         nc.sync.dma_start(out=q_sb[:, 2:4, :], in_=q_view[:, 2:4, :])
         nc.sync.dma_start(out=q_sb[:, 4:TILES, :], in_=q_view[:, 4:TILES, :])
-        nc.sync.dma_start(out=k_sb[1][:, 0:4, :], in_=k_views[1][:, 0:4, :])
-        nc.sync.dma_start(out=k_sb[1][:, 4:TILES, :], in_=k_views[1][:, 4:TILES, :])
         for c, stream in enumerate((sp, om1, om2)):
             nc.sync.dma_start(
                 out=om_sb[c][:].rearrange("p (a e) f -> p a e f", e=2),
@@ -108,10 +112,16 @@ def tile_sc_attn_pa_kernel(
             )
         nc.sync.dma_start(out=bias_bf[:], in_=v_b.partition_broadcast(P))
 
-        def weave(matmuls, transposes):
+        def weave(matmuls, transposes, lead=False):
             gaps = max(len(matmuls) - 1, 1)
             for m, (out, lhsT, rhs, start, stop) in enumerate(matmuls):
+                if lead:
+                    for n, (t_out, t_in, ident) in enumerate(transposes):
+                        if n * len(matmuls) // len(transposes) == m:
+                            nc.tensor.transpose(t_out, t_in, ident)
                 nc.tensor.matmul(out, lhsT=lhsT, rhs=rhs, start=start, stop=stop)
+                if lead:
+                    continue
                 for n, (t_out, t_in, ident) in enumerate(transposes):
                     if n * gaps // len(transposes) == m:
                         nc.tensor.transpose(t_out, t_in, ident)
@@ -122,31 +132,22 @@ def tile_sc_attn_pa_kernel(
         def work_bank(shape, dtype):
             return work_psum.tile(shape, dtype, name="work_bank", tag="work")
 
-        def key_transposes(j, h):
-            banks = [work_bank([P, 4, P], F32) for x in range(WORD_CHUNKS)]
-            calls = [
-                (banks[x][:, a, :], k_sb[j][:, 4 * h + a, :].bitcast(F32)[:, x * P : (x + 1) * P], ident_f32[:])
-                for x in range(WORD_CHUNKS)
-                for a in range(4)
-            ]
-            return banks, calls
-
-        def keep_key_transposes(j, h, banks, copiers):
-            for x, bank in enumerate(banks):
-                copiers[x % len(copiers)](
-                    out=kT[j][:, x, 512 * h : 512 * h + 512, :].rearrange("p k e -> p (k e)"),
-                    in_=bank[:].rearrange("p a k -> p (a k)").bitcast(BF16),
-                )
+        def turn_key2(part):
+            x, h = divmod(part, 2)
+            nc.vector.transpose(
+                out=k2T[:, x, 512 * h : 512 * h + 512, :].rearrange("p k e -> p (k e)").bitcast(F32),
+                in_=k2_blocks[:, x, 16 * h : 16 * h + 16, :].rearrange("p r d -> p (r d)").bitcast(F32),
+            )
 
         def transpose_key_tile(a, copier):
             bank = work_bank([P, WORD_CHUNKS, P], F32)
             for x in range(WORD_CHUNKS):
                 nc.tensor.transpose(
-                    bank[:, x, :], k_sb[0][:, a, :].bitcast(F32)[:, x * P : (x + 1) * P], ident_f32[:]
+                    bank[:, x, :], k1_sb[:, a, :].bitcast(F32)[:, x * P : (x + 1) * P], ident_f32[:]
                 )
             copier(
-                out=kT[0][:, :, a * P : (a + 1) * P, :].rearrange("p x k e -> p x (k e)"),
-                in_=bank[:].rearrange("p x k -> p (x k)").bitcast(BF16).rearrange("p (x k) -> p x k", x=WORD_CHUNKS),
+                out=k1T[:, a, :, :, :].rearrange("p x k e -> p (x k e)"),
+                in_=bank[:].rearrange("p x k -> p (x k)").bitcast(BF16),
             )
 
         def query_transposes(tiles):
@@ -235,11 +236,16 @@ def tile_sc_attn_pa_kernel(
                 score_psum.tile([P, 512], F32, name="score_bank", tag="scores") for h in range(PASSES)
             ]
             row_max[unit] = rotate.tile([P, PASSES], F32, name="row_max")
+            def keys(x, e, start):
+                if j == 0:
+                    return k1T[:, start // P : (start + width) // P, x, :, e]
+                return k2T[:, x, start : start + width, e].rearrange("p (a k) -> p a k", k=P)
+
             return [
                 (
-                    score_banks[unit][start // 512][:, start % 512 : start % 512 + width],
+                    score_banks[unit][start // 512][:, start % 512 : start % 512 + width].rearrange("p (a k) -> p a k", k=P),
                     qT[:, i, x, e, :],
-                    kT[j][:, x, start : start + width, e],
+                    keys(x, e, start),
                     (x, e) == (0, 0),
                     (x, e) == (WORD_CHUNKS - 1, 1),
                 )
@@ -348,6 +354,11 @@ def tile_sc_attn_pa_kernel(
             keep_query_transposes([i], bank, nc.scalar.copy)
             transpose_key_tile(i + 1, both[i % 2])
 
+        for x in range(WORD_CHUNKS):
+            for b in range(4):
+                d = 256 * x + 64 * b
+                (nc.scalar if K2_QUEUE == "scalar" else nc.sync).dma_start(out=k2_blocks[32 * b : 32 * b + 32, x, :, :], in_=k2_lanes[:, :, d : d + 64])
+
         x_grouped = {}
         turned_so_far = 0
         regrouped = []
@@ -356,12 +367,13 @@ def tile_sc_attn_pa_kernel(
             scored = step if step < UNITS else None
             multiplied = step - V_LAG if step >= V_LAG else None
             queries = QUERIES.get(step)
-            keys = (1, step - KEY2_START) if 0 <= step - KEY2_START < PASSES else None
             features = divmod(step - FEATURE_START, 2) if 0 <= step - FEATURE_START < FEATURE_STEPS else None
             quantised = divmod(step - FEATURE_START - 1, 2) if 0 <= step - FEATURE_START - 1 < FEATURE_STEPS else None
             values = step - VALUE_START if 0 <= step - VALUE_START < PASSES else None
             done_e = step - (E_LAG if step < UNITS else LATE_E_LAG)
             most = 0 if features is not None else CATCH_UP if values is not None else 1
+            if step >= UNITS:
+                most = UNITS if done_e >= UNITS - 1 else 0
             turned = list(range(turned_so_far, min(turned_so_far + most, done_e + 1, UNITS)))
             turned_so_far += len(turned)
 
@@ -372,9 +384,6 @@ def tile_sc_attn_pa_kernel(
             if multiplied is not None:
                 multiply_by_values(multiplied, LAST_PARTS if multiplied == UNITS - 1 else 1)
             transposes = []
-            if keys is not None:
-                key_banks, key_calls = key_transposes(keys[0], keys[1])
-                transposes.extend(key_calls)
             for unit in turned:
                 transposes.extend(e_transposes(unit))
             if features is not None:
@@ -393,7 +402,7 @@ def tile_sc_attn_pa_kernel(
                         rest = a - (TILES - HEAD_TILES)
                         weave(matmuls[4 * a : 4 * a + 4], transposes if rest == 0 else [])
             else:
-                weave(score_matmuls(scored) if scored is not None else [], transposes)
+                weave(score_matmuls(scored) if scored is not None else [], transposes, LEAD and features is not None)
 
             if values is not None:
                 quantise_values(values)
@@ -405,8 +414,6 @@ def tile_sc_attn_pa_kernel(
                 inverted_so_far += SUM_GROUP
             if multiplied is not None:
                 divide_and_store(multiplied, on_vector=(UNITS <= step < UNITS + LATE_E_LAG - E_LAG or (step > V_LATE and step % 2 == 0)))
-            if keys is not None:
-                keep_key_transposes(keys[0], keys[1], key_banks, both)
             if scored is not None:
                 half_maximum(scored, 0)
             for unit in turned:
@@ -416,8 +423,12 @@ def tile_sc_attn_pa_kernel(
                 nc.scalar.copy(out=copies[0][0], in_=copies[0][1])
             if queries is not None:
                 keep_query_transposes(queries, query_bank, nc.scalar.copy)
+            if features is not None and step in X_ON_SCALAR:
+                nc.scalar.copy(out=copies[1][0], in_=copies[1][1])
             if scored is not None:
                 half_maximum(scored, 1)
                 exponentials(scored)
-            if features is not None:
+            for part in [n for n in range(4) if KEY2_STEPS[n] == step]:
+                turn_key2(part)
+            if features is not None and step not in X_ON_SCALAR:
                 nc.vector.tensor_copy(out=copies[1][0], in_=copies[1][1])

@@ -24,10 +24,8 @@ PASSES = TOKENS // 512
 UNITS = 2 * TILES
 SCALE = 1.0 / math.sqrt(WIDTH)
 
-FEATURE_START = 3
-KEY2_STEPS = (4, 5, 6, 7)
-X_ON_SCALAR = (3, 4, 5, 6, 7, 8)
-K2_QUEUE = "scalar"
+KEY2_START = 1
+FEATURE_START = KEY2_START + PASSES
 FEATURE_STEPS = 2 * STREAMS
 VALUE_START = FEATURE_START + FEATURE_STEPS
 V_LAG = VALUE_START + PASSES
@@ -40,6 +38,8 @@ WARM = 6
 LAST_PARTS = 2
 V_LATE = 23
 LEAD = True
+V_COPIERS = ("scalar", "vector")
+X_ON_SCALAR = (3, 4, 5, 6, 7, 8)
 HEAD_TILES = 3
 QUERIES = {0: [2, 3], 1: [4, 5], 2: [6, 7]}
 WAITING = FEATURE_STEPS + E_LAG + 2
@@ -64,17 +64,17 @@ def tile_sc_attn_pa_kernel(
         ident_f32 = keep.tile([P, P], F32, name="ident_f32")
         zeros = keep.tile([P, WIDTH], BF16, name="zeros")
         q_sb = keep.tile([P, TILES, WIDTH], BF16, name="q_sb")
-        k1_sb = keep.tile([P, TILES, WIDTH], BF16, name="k1_sb")
-        k2_blocks = keep.tile([P, WORD_CHUNKS, TOKENS // 32, 64], BF16, name="k2_blocks", align_bytes=64)
+        k_sb = [keep.tile([P, TILES, WIDTH], BF16, name="k%d_sb" % j) for j in (1, 2)]
         om_sb = [keep.tile([P, TILES, WIDTH], BF16, name="om%d_sb" % c) for c in range(STREAMS)]
         qT = keep.tile([P, TILES, WORD_CHUNKS, 2, P], BF16, name="qT")
         k1T = keep.tile([P, TILES, WORD_CHUNKS, P, 2], BF16, name="k1T")
-        k2T = keep.tile([P, WORD_CHUNKS, TOKENS, 2], BF16, name="k2T", align_bytes=64)
+        k2T = keep.tile([P, WORD_CHUNKS, TOKENS, 2], BF16, name="k2T")
         bias_bf = keep.tile([P, WIDTH], BF16, name="bias_bf")
         w_words = keep.tile([P, STREAMS, WIDTH], U32, name="w_words", align_bytes=64)
         w_scales = keep.tile([P, STREAMS, WIDTH], U8, name="w_scales", align_bytes=64)
         x_words = keep.tile([P, STREAMS, TOKENS], U32, name="x_words", align_bytes=64)
         x_scales = keep.tile([P, STREAMS, TOKENS], U8, name="x_scales", align_bytes=64)
+        v_tiles = keep.tile([P, PASSES, 4, WIDTH], BF16, name="v_tiles", align_bytes=64)
         v_grouped = keep.tile([P, PASSES, WIDTH, 4], BF16, name="v_grouped", align_bytes=64)
         v_words = keep.tile([P, PASSES, WIDTH], U32, name="v_words", align_bytes=64)
         v_scales = keep.tile([P, PASSES, WIDTH], U8, name="v_scales", align_bytes=64)
@@ -87,15 +87,16 @@ def tile_sc_attn_pa_kernel(
         make_identity(nc, ident_f32[:])
         nc.vector.memset(w_scales[:].bitcast(I32), 0)
 
-        k1_view = k1.rearrange("(a p) d -> p a d", p=P)
-        k2_lanes = k2.rearrange("(r j) d -> j r d", j=32)
+        k_views = [k.rearrange("(a p) d -> p a d", p=P) for k in (k1, k2)]
         q_view = q.rearrange("(i p) d -> p i d", p=P)
-        nc.sync.dma_start(out=k1_sb[:, 0:1, :], in_=k1_view[:, 0:1, :])
+        nc.sync.dma_start(out=k_sb[0][:, 0:1, :], in_=k_views[0][:, 0:1, :])
         nc.sync.dma_start(out=q_sb[:, 0:2, :], in_=q_view[:, 0:2, :])
         for a in range(1, TILES):
-            nc.sync.dma_start(out=k1_sb[:, a : a + 1, :], in_=k1_view[:, a : a + 1, :])
+            nc.sync.dma_start(out=k_sb[0][:, a : a + 1, :], in_=k_views[0][:, a : a + 1, :])
         nc.sync.dma_start(out=q_sb[:, 2:4, :], in_=q_view[:, 2:4, :])
         nc.sync.dma_start(out=q_sb[:, 4:TILES, :], in_=q_view[:, 4:TILES, :])
+        nc.sync.dma_start(out=k_sb[1][:, 0:4, :], in_=k_views[1][:, 0:4, :])
+        nc.sync.dma_start(out=k_sb[1][:, 4:TILES, :], in_=k_views[1][:, 4:TILES, :])
         for c, stream in enumerate((sp, om1, om2)):
             nc.sync.dma_start(
                 out=om_sb[c][:].rearrange("p (a e) f -> p a e f", e=2),
@@ -132,18 +133,27 @@ def tile_sc_attn_pa_kernel(
         def work_bank(shape, dtype):
             return work_psum.tile(shape, dtype, name="work_bank", tag="work")
 
-        def turn_key2(part):
-            x, h = divmod(part, 2)
-            nc.vector.transpose(
-                out=k2T[:, x, 512 * h : 512 * h + 512, :].rearrange("p k e -> p (k e)").bitcast(F32),
-                in_=k2_blocks[:, x, 16 * h : 16 * h + 16, :].rearrange("p r d -> p (r d)").bitcast(F32),
-            )
+        def key_transposes(j, h):
+            banks = [work_bank([P, 4, P], F32) for x in range(WORD_CHUNKS)]
+            calls = [
+                (banks[x][:, a, :], k_sb[j][:, 4 * h + a, :].bitcast(F32)[:, x * P : (x + 1) * P], ident_f32[:])
+                for x in range(WORD_CHUNKS)
+                for a in range(4)
+            ]
+            return banks, calls
+
+        def keep_key_transposes(j, h, banks, copiers):
+            for x, bank in enumerate(banks):
+                copiers[x % len(copiers)](
+                    out=k2T[:, x, 512 * h : 512 * h + 512, :].rearrange("p k e -> p (k e)"),
+                    in_=bank[:].rearrange("p a k -> p (a k)").bitcast(BF16),
+                )
 
         def transpose_key_tile(a, copier):
             bank = work_bank([P, WORD_CHUNKS, P], F32)
             for x in range(WORD_CHUNKS):
                 nc.tensor.transpose(
-                    bank[:, x, :], k1_sb[:, a, :].bitcast(F32)[:, x * P : (x + 1) * P], ident_f32[:]
+                    bank[:, x, :], k_sb[0][:, a, :].bitcast(F32)[:, x * P : (x + 1) * P], ident_f32[:]
                 )
             copier(
                 out=k1T[:, a, :, :, :].rearrange("p x k e -> p (x k e)"),
@@ -194,34 +204,36 @@ def tile_sc_attn_pa_kernel(
             )
 
         def project_values(g):
-            for n in range(CHUNKS):
-                columns = slice(n * P, (n + 1) * P)
-                bank = work_bank([P, 4, P], F32)
-                for t in range(4):
-                    tokens = slice((4 * g + t) * P, (4 * g + t + 1) * P)
-                    for c in range(STREAMS):
-                        nc.tensor.matmul_mx(
-                            out=bank[:, t, :],
-                            lhsT=x_words[:, c, tokens].bitcast(FP8X4),
-                            lhsT_scale=x_scales[:, c, tokens],
-                            rhs=w_words[:, c, columns].bitcast(FP8X4),
-                            rhs_scale=w_scales[:, c, columns],
-                            start=(c == 0),
-                            stop=(c == STREAMS - 1),
-                        )
-                nc.vector.tensor_tensor(
-                    out=v_grouped[:, g, columns, :],
-                    in0=bank[:].rearrange("p t n -> p n t"),
-                    in1=bias_bf[:, columns].unsqueeze(2).to_broadcast([P, P, 4]),
-                    op=ALU.add,
+            for t in range(4):
+                tokens = slice((4 * g + t) * P, (4 * g + t + 1) * P)
+                bank = work_bank([P, WIDTH], F32)
+                for c in range(STREAMS):
+                    nc.tensor.matmul_mx(
+                        out=bank[:],
+                        lhsT=x_words[:, c, tokens].bitcast(FP8X4),
+                        lhsT_scale=x_scales[:, c, tokens],
+                        rhs=w_words[:, c, :].bitcast(FP8X4),
+                        rhs_scale=w_scales[:, c, :],
+                        start=(c == 0),
+                        stop=(c == STREAMS - 1),
+                    )
+                nc.vector.tensor_tensor(out=v_tiles[:, g, t, :], in0=bank[:], in1=bias_bf[:], op=ALU.add)
+
+        def group_values(g):
+            for half, copier in enumerate(V_COPIERS):
+                columns = slice(256 * half, 256 * half + 256)
+                (nc.scalar.copy if copier == "scalar" else nc.vector.tensor_copy)(
+                    out=v_grouped[:, g, columns, :], in_=v_tiles[:, g, :, columns].rearrange("p t n -> p n t")
                 )
 
         def quantise_values(g):
-            nc.vector.quantize_mx(
-                out=v_words[:, g, :].bitcast(FP8X4),
-                scales=v_scales[:, g, :],
-                in_=v_grouped[:, g, :, :].rearrange("p n t -> p (n t)"),
-            )
+            for half in range(2):
+                columns = slice(256 * half, 256 * half + 256)
+                nc.vector.quantize_mx(
+                    out=v_words[:, g, columns].bitcast(FP8X4),
+                    scales=v_scales[:, g, columns],
+                    in_=v_grouped[:, g, columns, :].rearrange("p n t -> p (n t)"),
+                )
 
         score_banks = {}
         row_max = {}
@@ -354,11 +366,6 @@ def tile_sc_attn_pa_kernel(
             keep_query_transposes([i], bank, nc.scalar.copy)
             transpose_key_tile(i + 1, both[i % 2])
 
-        for x in range(WORD_CHUNKS):
-            for b in range(4):
-                d = 256 * x + 64 * b
-                (nc.scalar if K2_QUEUE == "scalar" else nc.sync).dma_start(out=k2_blocks[32 * b : 32 * b + 32, x, :, :], in_=k2_lanes[:, :, d : d + 64])
-
         x_grouped = {}
         turned_so_far = 0
         regrouped = []
@@ -367,6 +374,7 @@ def tile_sc_attn_pa_kernel(
             scored = step if step < UNITS else None
             multiplied = step - V_LAG if step >= V_LAG else None
             queries = QUERIES.get(step)
+            keys = (1, step - KEY2_START) if 0 <= step - KEY2_START < PASSES else None
             features = divmod(step - FEATURE_START, 2) if 0 <= step - FEATURE_START < FEATURE_STEPS else None
             quantised = divmod(step - FEATURE_START - 1, 2) if 0 <= step - FEATURE_START - 1 < FEATURE_STEPS else None
             values = step - VALUE_START if 0 <= step - VALUE_START < PASSES else None
@@ -384,6 +392,9 @@ def tile_sc_attn_pa_kernel(
             if multiplied is not None:
                 multiply_by_values(multiplied, LAST_PARTS if multiplied == UNITS - 1 else 1)
             transposes = []
+            if keys is not None:
+                key_banks, key_calls = key_transposes(keys[0], keys[1])
+                transposes.extend(key_calls)
             for unit in turned:
                 transposes.extend(e_transposes(unit))
             if features is not None:
@@ -405,6 +416,7 @@ def tile_sc_attn_pa_kernel(
                 weave(score_matmuls(scored) if scored is not None else [], transposes, LEAD and features is not None)
 
             if values is not None:
+                group_values(values)
                 quantise_values(values)
             for unit in regrouped[:QUANTISES]:
                 quantise_e(unit)
@@ -414,6 +426,8 @@ def tile_sc_attn_pa_kernel(
                 inverted_so_far += SUM_GROUP
             if multiplied is not None:
                 divide_and_store(multiplied, on_vector=(UNITS <= step < UNITS + LATE_E_LAG - E_LAG or (step > V_LATE and step % 2 == 0)))
+            if keys is not None:
+                keep_key_transposes(keys[0], keys[1], key_banks, both)
             if scored is not None:
                 half_maximum(scored, 0)
             for unit in turned:
@@ -428,7 +442,5 @@ def tile_sc_attn_pa_kernel(
             if scored is not None:
                 half_maximum(scored, 1)
                 exponentials(scored)
-            for part in [n for n in range(4) if KEY2_STEPS[n] == step]:
-                turn_key2(part)
             if features is not None and step not in X_ON_SCALAR:
                 nc.vector.tensor_copy(out=copies[1][0], in_=copies[1][1])

@@ -38,7 +38,8 @@ WARM = 6
 LAST_PARTS = 2
 V_LATE = 23
 LEAD = True
-V_COPIERS = ("scalar", "vector")
+PV_LAST = True
+V_COPIERS = ("vector", "vector")
 X_ON_SCALAR = (3, 4, 5, 6, 7, 8)
 HEAD_TILES = 3
 QUERIES = {0: [2, 3], 1: [4, 5], 2: [6, 7]}
@@ -66,7 +67,7 @@ def tile_sc_attn_pa_kernel(
         q_sb = keep.tile([P, TILES, WIDTH], BF16, name="q_sb")
         k_sb = [keep.tile([P, TILES, WIDTH], BF16, name="k%d_sb" % j) for j in (1, 2)]
         om_sb = [keep.tile([P, TILES, WIDTH], BF16, name="om%d_sb" % c) for c in range(STREAMS)]
-        qT = keep.tile([P, TILES, WORD_CHUNKS, 2, P], BF16, name="qT")
+        qT = keep.tile([P, TILES, WORD_CHUNKS, P, 2], BF16, name="qT")
         k1T = keep.tile([P, TILES, WORD_CHUNKS, P, 2], BF16, name="k1T")
         k2T = keep.tile([P, WORD_CHUNKS, TOKENS, 2], BF16, name="k2T")
         bias_bf = keep.tile([P, WIDTH], BF16, name="bias_bf")
@@ -171,8 +172,8 @@ def tile_sc_attn_pa_kernel(
 
         def keep_query_transposes(tiles, bank, copier):
             copier(
-                out=qT[:, tiles[0] : tiles[-1] + 1, :, :, :].rearrange("p i x e m -> p (i x) e m"),
-                in_=bank[:].rearrange("p i x m -> p (i x m)").bitcast(BF16).rearrange("p (c m e) -> p c e m", m=P, e=2),
+                out=qT[:, tiles[0] : tiles[-1] + 1, :, :, :].rearrange("p i x m e -> p (i x m e)"),
+                in_=bank[:].rearrange("p i x m -> p (i x m)").bitcast(BF16),
             )
 
         def feature_transposes(c, half):
@@ -256,7 +257,7 @@ def tile_sc_attn_pa_kernel(
             return [
                 (
                     score_banks[unit][start // 512][:, start % 512 : start % 512 + width].rearrange("p (a k) -> p a k", k=P),
-                    qT[:, i, x, e, :],
+                    qT[:, i, x, :, e],
                     keys(x, e, start),
                     (x, e) == (0, 0),
                     (x, e) == (WORD_CHUNKS - 1, 1),
@@ -389,7 +390,7 @@ def tile_sc_attn_pa_kernel(
                 quantise_features(quantised[0], quantised[1], x_grouped[step - 1])
             if values is not None:
                 project_values(values)
-            if multiplied is not None:
+            if multiplied is not None and not PV_LAST:
                 multiply_by_values(multiplied, LAST_PARTS if multiplied == UNITS - 1 else 1)
             transposes = []
             if keys is not None:
@@ -414,6 +415,8 @@ def tile_sc_attn_pa_kernel(
                         weave(matmuls[4 * a : 4 * a + 4], transposes if rest == 0 else [])
             else:
                 weave(score_matmuls(scored) if scored is not None else [], transposes, LEAD and features is not None)
+            if multiplied is not None and PV_LAST:
+                multiply_by_values(multiplied, LAST_PARTS if multiplied == UNITS - 1 else 1)
 
             if values is not None:
                 group_values(values)
@@ -436,7 +439,7 @@ def tile_sc_attn_pa_kernel(
                 x_grouped[step], copies = regroup_features(feature_banks)
                 nc.scalar.copy(out=copies[0][0], in_=copies[0][1])
             if queries is not None:
-                keep_query_transposes(queries, query_bank, nc.scalar.copy)
+                keep_query_transposes(queries, query_bank, nc.vector.tensor_copy)
             if features is not None and step in X_ON_SCALAR:
                 nc.scalar.copy(out=copies[1][0], in_=copies[1][1])
             if scored is not None:

@@ -34,7 +34,7 @@ LATE_E_LAG = 5
 CATCH_UP = (FEATURE_STEPS + PASSES) // PASSES
 QUANTISES = 2
 SUM_GROUP = 4
-WARM = 6
+WARM = 3
 LAST_PARTS = 2
 V_LATE = 23
 LEAD = True
@@ -418,9 +418,6 @@ def tile_sc_attn_pa_kernel(
             if multiplied is not None and PV_LAST:
                 multiply_by_values(multiplied, LAST_PARTS if multiplied == UNITS - 1 else 1)
 
-            if values is not None:
-                group_values(values)
-                quantise_values(values)
             for unit in regrouped[:QUANTISES]:
                 quantise_e(unit)
             regrouped = regrouped[QUANTISES:] + turned
@@ -433,6 +430,9 @@ def tile_sc_attn_pa_kernel(
                 keep_key_transposes(keys[0], keys[1], key_banks, both)
             if scored is not None:
                 half_maximum(scored, 0)
+            if values is not None:
+                group_values(values)
+                quantise_values(values)
             for unit in turned:
                 regroup_e(unit, nc.scalar.copy if values is not None else nc.vector.tensor_copy)
             if features is not None:

from contextlib import ExitStack
import math

import concourse.mybir as mybir
from concourse.masks import make_identity

BF16 = mybir.dt.bfloat16
F32 = mybir.dt.float32
I32 = mybir.dt.int32
U32 = mybir.dt.uint32
U8 = mybir.dt.uint8
FP8X4 = mybir.dt.float8_e4m3fn_x4
ALU = mybir.AluOpType
ACT = mybir.ActivationFunctionType

P = 128
TOKENS = 1024
WIDTH = 512
STREAMS = 3
TILES = TOKENS // P
CHUNKS = WIDTH // P
WORD_CHUNKS = WIDTH // 2 // P
PASSES = TOKENS // 512
UNITS = 2 * TILES
SCALE = 1.0 / math.sqrt(WIDTH)

KEY2_START = 1
FEATURE_START = KEY2_START + PASSES
FEATURE_STEPS = 2 * STREAMS
VALUE_START = FEATURE_START + FEATURE_STEPS
V_LAG = VALUE_START + PASSES
E_LAG = 2
LATE_E_LAG = 5
CATCH_UP = (FEATURE_STEPS + PASSES) // PASSES
QUANTISES = 2
SUM_GROUP = 4
WARM = 3
LAST_PARTS = 2
V_LATE = 23
LEAD = True
PV_LAST = True
V_COPIERS = ("vector", "vector")
X_ON_SCALAR = (3, 4, 5, 6, 7, 8)
HEAD_TILES = 3
QUERIES = {0: [2, 3], 1: [4, 5], 2: [6, 7]}
WAITING = FEATURE_STEPS + E_LAG + 2

FLOPS = 2 * TOKENS * STREAMS * WIDTH * WIDTH + 2 * 2 * (2 * TOKENS * TOKENS * WIDTH)


def tile_sc_attn_pa_kernel(
    tc, q, k1, k2, sp, om1, om2, v_w_words, v_w_scales, v_b, out_0, out_1
):
    nc = tc.nc
    outs = (out_0, out_1)
    with ExitStack() as ctx:
        keep = ctx.enter_context(tc.tile_pool(name="keep", bufs=1))
        rotate = ctx.enter_context(tc.tile_pool(name="rotate", bufs=4))
        results = ctx.enter_context(tc.tile_pool(name="results", bufs=V_LAG))
        waiting = ctx.enter_context(tc.tile_pool(name="waiting", bufs=WAITING))
        score_psum = ctx.enter_context(tc.psum_pool(name="score_psum", bufs=4))
        work_psum = ctx.enter_context(tc.psum_pool(name="work_psum", bufs=4))
        ctx.enter_context(tc.manual_schedule())

        ident_f32 = keep.tile([P, P], F32, name="ident_f32")
        zeros = keep.tile([P, WIDTH], BF16, name="zeros")
        q_sb = keep.tile([P, TILES, WIDTH], BF16, name="q_sb")
        k_sb = [keep.tile([P, TILES, WIDTH], BF16, name="k%d_sb" % j) for j in (1, 2)]
        om_sb = [keep.tile([P, TILES, WIDTH], BF16, name="om%d_sb" % c) for c in range(STREAMS)]
        qT = keep.tile([P, TILES, WORD_CHUNKS, P, 2], BF16, name="qT")
        k1T = keep.tile([P, TILES, WORD_CHUNKS, P, 2], BF16, name="k1T")
        k2T = keep.tile([P, WORD_CHUNKS, TOKENS, 2], BF16, name="k2T")
        bias_bf = keep.tile([P, WIDTH], BF16, name="bias_bf")
        w_words = keep.tile([P, STREAMS, WIDTH], U32, name="w_words", align_bytes=64)
        w_scales = keep.tile([P, STREAMS, WIDTH], U8, name="w_scales", align_bytes=64)
        x_words = keep.tile([P, STREAMS, TOKENS], U32, name="x_words", align_bytes=64)
        x_scales = keep.tile([P, STREAMS, TOKENS], U8, name="x_scales", align_bytes=64)
        v_tiles = keep.tile([P, PASSES, 4, WIDTH], BF16, name="v_tiles", align_bytes=64)
        v_grouped = keep.tile([P, PASSES, WIDTH, 4], BF16, name="v_grouped", align_bytes=64)
        v_words = keep.tile([P, PASSES, WIDTH], U32, name="v_words", align_bytes=64)
        v_scales = keep.tile([P, PASSES, WIDTH], U8, name="v_scales", align_bytes=64)
        e_words = keep.tile([P, UNITS, PASSES * P], U32, name="e_words", align_bytes=64)
        e_scales = keep.tile([P, UNITS, PASSES * P], U8, name="e_scales", align_bytes=64)
        e_sums = keep.tile([P, UNITS, PASSES], F32, name="e_sums")
        inv_sum = keep.tile([P, UNITS], F32, name="inv_sum")

        nc.vector.memset(zeros[:], 0.0)
        make_identity(nc, ident_f32[:])
        nc.vector.memset(w_scales[:].bitcast(I32), 0)

        k_views = [k.rearrange("(a p) d -> p a d", p=P) for k in (k1, k2)]
        q_view = q.rearrange("(i p) d -> p i d", p=P)
        nc.sync.dma_start(out=k_sb[0][:, 0:1, :], in_=k_views[0][:, 0:1, :])
        nc.sync.dma_start(out=q_sb[:, 0:2, :], in_=q_view[:, 0:2, :])
        for a in range(1, TILES):
            nc.sync.dma_start(out=k_sb[0][:, a : a + 1, :], in_=k_views[0][:, a : a + 1, :])
        nc.sync.dma_start(out=q_sb[:, 2:4, :], in_=q_view[:, 2:4, :])
        nc.sync.dma_start(out=q_sb[:, 4:TILES, :], in_=q_view[:, 4:TILES, :])
        nc.sync.dma_start(out=k_sb[1][:, 0:4, :], in_=k_views[1][:, 0:4, :])
        nc.sync.dma_start(out=k_sb[1][:, 4:TILES, :], in_=k_views[1][:, 4:TILES, :])
        for c, stream in enumerate((sp, om1, om2)):
            nc.sync.dma_start(
                out=om_sb[c][:].rearrange("p (a e) f -> p a e f", e=2),
                in_=stream.rearrange("(a p e) f -> p a e f", p=P, e=2),
            )
        nc.sync.dma_start(
            out=w_words[:].bitcast(I32),
            in_=v_w_words.rearrange("c p n t -> p c (n t)").bitcast(I32),
        )
        for quadrant in range(4):
            nc.sync.dma_start(
                out=w_scales[32 * quadrant : 32 * quadrant + 4, :, :].bitcast(I32),
                in_=v_w_scales[:, 4 * quadrant : 4 * quadrant + 4, :].rearrange("c r n -> r c n").bitcast(I32),
            )
        nc.sync.dma_start(out=bias_bf[:], in_=v_b.partition_broadcast(P))

        def weave(matmuls, transposes, lead=False):
            gaps = max(len(matmuls) - 1, 1)
            for m, (out, lhsT, rhs, start, stop) in enumerate(matmuls):
                if lead:
                    for n, (t_out, t_in, ident) in enumerate(transposes):
                        if n * len(matmuls) // len(transposes) == m:
                            nc.tensor.transpose(t_out, t_in, ident)
                nc.tensor.matmul(out, lhsT=lhsT, rhs=rhs, start=start, stop=stop)
                if lead:
                    continue
                for n, (t_out, t_in, ident) in enumerate(transposes):
                    if n * gaps // len(transposes) == m:
                        nc.tensor.transpose(t_out, t_in, ident)
            if not matmuls:
                for t_out, t_in, ident in transposes:
                    nc.tensor.transpose(t_out, t_in, ident)

        def work_bank(shape, dtype):
            return work_psum.tile(shape, dtype, name="work_bank", tag="work")

        def key_transposes(j, h):
            banks = [work_bank([P, 4, P], F32) for x in range(WORD_CHUNKS)]
            calls = [
                (banks[x][:, a, :], k_sb[j][:, 4 * h + a, :].bitcast(F32)[:, x * P : (x + 1) * P], ident_f32[:])
                for x in range(WORD_CHUNKS)
                for a in range(4)
            ]
            return banks, calls

        def keep_key_transposes(j, h, banks, copiers):
            for x, bank in enumerate(banks):
                copiers[x % len(copiers)](
                    out=k2T[:, x, 512 * h : 512 * h + 512, :].rearrange("p k e -> p (k e)"),
                    in_=bank[:].rearrange("p a k -> p (a k)").bitcast(BF16),
                )

        def transpose_key_tile(a, copier):
            bank = work_bank([P, WORD_CHUNKS, P], F32)
            for x in range(WORD_CHUNKS):
                nc.tensor.transpose(
                    bank[:, x, :], k_sb[0][:, a, :].bitcast(F32)[:, x * P : (x + 1) * P], ident_f32[:]
                )
            copier(
                out=k1T[:, a, :, :, :].rearrange("p x k e -> p (x k e)"),
                in_=bank[:].rearrange("p x k -> p (x k)").bitcast(BF16),
            )

        def query_transposes(tiles):
            bank = work_bank([P, len(tiles), WORD_CHUNKS, P], F32)
            calls = [
                (bank[:, n, x, :], q_sb[:, i, :].bitcast(F32)[:, x * P : (x + 1) * P], ident_f32[:])
                for n, i in enumerate(tiles)
                for x in range(WORD_CHUNKS)
            ]
            return bank, calls

        def keep_query_transposes(tiles, bank, copier):
            copier(
                out=qT[:, tiles[0] : tiles[-1] + 1, :, :, :].rearrange("p i x m e -> p (i x m e)"),
                in_=bank[:].rearrange("p i x m -> p (i x m)").bitcast(BF16),
            )

        def feature_transposes(c, half):
            banks = [work_bank([P, 2, 2, P], F32) for b in range(2)]
            calls = [
                (
                    banks[b][:, a, u, :],
                    om_sb[c][:, 4 * half + 2 * b + a, :].bitcast(F32)[:, u : WIDTH // 2 : 2],
                    ident_f32[:],
                )
                for b in range(2)
                for a in range(2)
                for u in range(2)
            ]
            return banks, calls

        def regroup_features(banks):
            grouped = rotate.tile([P, 4 * P * 4], BF16, name="x_grouped", align_bytes=64)
            words = grouped[:].bitcast(F32).rearrange("p (a k u) -> p a k u", a=4, u=2)
            return grouped, [
                (words[:, 2 * b : 2 * b + 2, :, :], bank[:].rearrange("p a u k -> p a k u"))
                for b, bank in enumerate(banks)
            ]

        def quantise_features(c, half, grouped):
            columns = slice(512 * half, 512 * half + 512)
            nc.vector.quantize_mx(
                out=x_words[:, c, columns].bitcast(FP8X4), scales=x_scales[:, c, columns], in_=grouped[:]
            )

        def project_values(g):
            for t in range(4):
                tokens = slice((4 * g + t) * P, (4 * g + t + 1) * P)
                bank = work_bank([P, WIDTH], F32)
                for c in range(STREAMS):
                    nc.tensor.matmul_mx(
                        out=bank[:],
                        lhsT=x_words[:, c, tokens].bitcast(FP8X4),
                        lhsT_scale=x_scales[:, c, tokens],
                        rhs=w_words[:, c, :].bitcast(FP8X4),
                        rhs_scale=w_scales[:, c, :],
                        start=(c == 0),
                        stop=(c == STREAMS - 1),
                    )
                nc.vector.tensor_tensor(out=v_tiles[:, g, t, :], in0=bank[:], in1=bias_bf[:], op=ALU.add)

        def group_values(g):
            for half, copier in enumerate(V_COPIERS):
                columns = slice(256 * half, 256 * half + 256)
                (nc.scalar.copy if copier == "scalar" else nc.vector.tensor_copy)(
                    out=v_grouped[:, g, columns, :], in_=v_tiles[:, g, :, columns].rearrange("p t n -> p n t")
                )

        def quantise_values(g):
            for half in range(2):
                columns = slice(256 * half, 256 * half + 256)
                nc.vector.quantize_mx(
                    out=v_words[:, g, columns].bitcast(FP8X4),
                    scales=v_scales[:, g, columns],
                    in_=v_grouped[:, g, columns, :].rearrange("p n t -> p (n t)"),
                )

        score_banks = {}
        row_max = {}
        e_rows = {}
        e_banks = {}
        e_grouped = {}
        products = {}

        def score_matmuls(unit, width=512):
            j, i = divmod(unit, TILES)
            score_banks[unit] = [
                score_psum.tile([P, 512], F32, name="score_bank", tag="scores") for h in range(PASSES)
            ]
            row_max[unit] = rotate.tile([P, PASSES], F32, name="row_max")
            def keys(x, e, start):
                if j == 0:
                    return k1T[:, start // P : (start + width) // P, x, :, e]
                return k2T[:, x, start : start + width, e].rearrange("p (a k) -> p a k", k=P)

            return [
                (
                    score_banks[unit][start // 512][:, start % 512 : start % 512 + width].rearrange("p (a k) -> p a k", k=P),
                    qT[:, i, x, :, e],
                    keys(x, e, start),
                    (x, e) == (0, 0),
                    (x, e) == (WORD_CHUNKS - 1, 1),
                )
                for start in range(0, TOKENS, width)
                for x in range(WORD_CHUNKS)
                for e in range(2)
            ]

        def half_maximum(unit, h):
            nc.vector.tensor_reduce(
                out=row_max[unit][:, h : h + 1], in_=score_banks[unit][h][:], axis=mybir.AxisListType.X, op=ALU.max
            )

        def exponentials(unit):
            shift = rotate.tile([P, 1], F32, name="shift")
            nc.vector.tensor_scalar(
                out=shift[:],
                in0=row_max[unit][:, 0:1],
                scalar1=row_max[unit][:, 1:2],
                scalar2=-SCALE,
                op0=ALU.max,
                op1=ALU.mult,
            )
            e_rows[unit] = waiting.tile([P, TOKENS], BF16, name="e_rows")
            for h in range(PASSES):
                nc.scalar.activation(
                    out=e_rows[unit][:, 512 * h : 512 * h + 512],
                    in_=score_banks[unit][h][:],
                    func=ACT.Exp,
                    bias=shift[:, 0:1],
                    scale=SCALE,
                    accum_out=e_sums[:, unit, h : h + 1],
                )

        def e_transposes(unit):
            e_banks[unit] = work_bank([P, 2 * PASSES, P], F32)
            pairs = e_rows[unit][:].bitcast(F32)
            return [
                (e_banks[unit][:, x, :], pairs[:, x * P : (x + 1) * P], ident_f32[:])
                for x in range(2 * PASSES)
            ]

        def regroup_e(unit, copier):
            e_grouped[unit] = waiting.tile([P, PASSES * P * 4], BF16, name="e_grouped", align_bytes=64)
            copier(
                out=e_grouped[unit][:].bitcast(F32).rearrange("p (g m u) -> p g m u", g=PASSES, u=2),
                in_=e_banks[unit][:].rearrange("p (g u) m -> p g m u", u=2),
            )

        def quantise_e(unit):
            nc.vector.quantize_mx(
                out=e_words[:, unit, :].bitcast(FP8X4), scales=e_scales[:, unit, :], in_=e_grouped[unit][:]
            )

        def invert_sums(units):
            total = rotate.tile([P, SUM_GROUP], F32, name="total")
            nc.vector.tensor_reduce(out=total[:], in_=e_sums[:, units, :], axis=mybir.AxisListType.X, op=ALU.add)
            nc.vector.reciprocal(out=inv_sum[:, units], in_=total[:])

        def multiply_by_values(unit, parts):
            width = WIDTH // parts
            products[unit] = []
            for n in range(parts):
                columns = slice(n * width, (n + 1) * width)
                bank = work_bank([P, WIDTH], F32)
                products[unit].append((columns, bank))
                for g in range(PASSES):
                    queries = slice(g * P, (g + 1) * P)
                    nc.tensor.matmul_mx(
                        out=bank[:, 0:width],
                        lhsT=e_words[:, unit, queries].bitcast(FP8X4),
                        lhsT_scale=e_scales[:, unit, queries],
                        rhs=v_words[:, g, columns].bitcast(FP8X4),
                        rhs_scale=v_scales[:, g, columns],
                        start=(g == 0),
                        stop=(g == PASSES - 1),
                    )

        def divide_and_store(unit, on_vector):
            j, i = divmod(unit, TILES)
            for n, (columns, bank) in enumerate(products[unit]):
                width = columns.stop - columns.start
                attn = results.tile([P, WIDTH], F32, name="attn")
                if on_vector == (n == 0):
                    nc.vector.tensor_scalar(
                        out=attn[:, 0:width],
                        in0=bank[:, 0:width],
                        scalar1=inv_sum[:, unit : unit + 1],
                        scalar2=None,
                        op0=ALU.mult,
                    )
                else:
                    nc.scalar.activation(
                        out=attn[:, 0:width], in_=bank[:, 0:width], func=ACT.Copy, scale=inv_sum[:, unit : unit + 1]
                    )
                nc.sync.dma_start(out=outs[j][i * P : (i + 1) * P, columns], in_=attn[:, 0:width])

        both = (nc.vector.tensor_copy, nc.scalar.copy)
        warm_bank = work_bank([P, WIDTH], F32)
        for repeat in range(WARM):
            nc.tensor.matmul(warm_bank[:], lhsT=zeros[:, 0:P], rhs=zeros[:], start=True, stop=True)
        transpose_key_tile(0, nc.vector.tensor_copy)
        for i in range(2):
            bank, calls = query_transposes([i])
            weave([], calls)
            keep_query_transposes([i], bank, nc.scalar.copy)
            transpose_key_tile(i + 1, both[i % 2])

        x_grouped = {}
        turned_so_far = 0
        regrouped = []
        inverted_so_far = 0
        for step in range(UNITS + V_LAG):
            scored = step if step < UNITS else None
            multiplied = step - V_LAG if step >= V_LAG else None
            queries = QUERIES.get(step)
            keys = (1, step - KEY2_START) if 0 <= step - KEY2_START < PASSES else None
            features = divmod(step - FEATURE_START, 2) if 0 <= step - FEATURE_START < FEATURE_STEPS else None
            quantised = divmod(step - FEATURE_START - 1, 2) if 0 <= step - FEATURE_START - 1 < FEATURE_STEPS else None
            values = step - VALUE_START if 0 <= step - VALUE_START < PASSES else None
            done_e = step - (E_LAG if step < UNITS else LATE_E_LAG)
            most = 0 if features is not None else CATCH_UP if values is not None else 1
            if step >= UNITS:
                most = UNITS if done_e >= UNITS - 1 else 0
            turned = list(range(turned_so_far, min(turned_so_far + most, done_e + 1, UNITS)))
            turned_so_far += len(turned)

            if quantised is not None:
                quantise_features(quantised[0], quantised[1], x_grouped[step - 1])
            if values is not None:
                project_values(values)
            if multiplied is not None and not PV_LAST:
                multiply_by_values(multiplied, LAST_PARTS if multiplied == UNITS - 1 else 1)
            transposes = []
            if keys is not None:
                key_banks, key_calls = key_transposes(keys[0], keys[1])
                transposes.extend(key_calls)
            for unit in turned:
                transposes.extend(e_transposes(unit))
            if features is not None:
                feature_banks, calls = feature_transposes(features[0], features[1])
                transposes.extend(calls)
            if queries is not None:
                query_bank, calls = query_transposes(queries)
                transposes.extend(calls)
            if step == 0:
                matmuls = score_matmuls(0, P)
                for a in range(TILES):
                    if a + HEAD_TILES < TILES:
                        weave(matmuls[4 * a : 4 * a + 4], [])
                        transpose_key_tile(a + HEAD_TILES, both[(a + HEAD_TILES) % 2])
                    else:
                        rest = a - (TILES - HEAD_TILES)
                        weave(matmuls[4 * a : 4 * a + 4], transposes if rest == 0 else [])
            else:
                weave(score_matmuls(scored) if scored is not None else [], transposes, LEAD and features is not None)
            if multiplied is not None and PV_LAST:
                multiply_by_values(multiplied, LAST_PARTS if multiplied == UNITS - 1 else 1)

            for unit in regrouped[:QUANTISES]:
                quantise_e(unit)
            regrouped = regrouped[QUANTISES:] + turned
            if inverted_so_far + SUM_GROUP <= min(done_e + 1, UNITS):
                invert_sums(slice(inverted_so_far, inverted_so_far + SUM_GROUP))
                inverted_so_far += SUM_GROUP
            if multiplied is not None:
                divide_and_store(multiplied, on_vector=(UNITS <= step < UNITS + LATE_E_LAG - E_LAG or (step > V_LATE and step % 2 == 0)))
            if keys is not None:
                keep_key_transposes(keys[0], keys[1], key_banks, both)
            if scored is not None:
                half_maximum(scored, 0)
            if values is not None:
                group_values(values)
                quantise_values(values)
            for unit in turned:
                regroup_e(unit, nc.scalar.copy if values is not None else nc.vector.tensor_copy)
            if features is not None:
                x_grouped[step], copies = regroup_features(feature_banks)
                nc.scalar.copy(out=copies[0][0], in_=copies[0][1])
            if queries is not None:
                keep_query_transposes(queries, query_bank, nc.vector.tensor_copy)
            if features is not None and step in X_ON_SCALAR:
                nc.scalar.copy(out=copies[1][0], in_=copies[1][1])
            if scored is not None:
                half_maximum(scored, 1)
                exponentials(scored)
            if features is not None and step not in X_ON_SCALAR:
                nc.vector.tensor_copy(out=copies[1][0], in_=copies[1][1])
